import numpy as np
import ml_dtypes


def mxq(x, axis, fmt="e4m3"):
    dtype, down = {"e4m3": (ml_dtypes.float8_e4m3fn, 7), "e5m2": (ml_dtypes.float8_e5m2, 14)}[fmt]
    v = np.moveaxis(np.asarray(x, np.float32).astype(ml_dtypes.bfloat16).astype(np.float64), axis, -1)
    blocks = v.reshape(v.shape[:-1] + (-1, 32))
    amax = np.abs(blocks).max(-1, keepdims=True)
    byte = np.maximum(np.where(amax > 0, np.frexp(amax)[1] - 1 + 127, 0) - down, 1)
    scale = np.exp2(byte - 127.0)
    codes = (blocks / scale).astype(np.float32).astype(dtype).astype(np.float64)
    return np.moveaxis((codes * scale).reshape(v.shape), -1, axis)


WIDE = False


def mx_kscale(k):
    if not WIDE:
        return np.ones(k)
    levels = np.array([10, -10, 5, -5, 0])
    a = np.random.permutation(np.resize(levels, k // 512 * 4)).reshape(k // 512, 4)
    idx = np.arange(k)
    return np.exp2(a[idx // 512, idx % 128 // 32])


BF16 = ml_dtypes.bfloat16


def bf(x):
    return np.asarray(x, np.float32).astype(BF16)


def f64(x):
    return np.asarray(x).astype(np.float64)


B, T, D, N, L, H = 128, 64, 512, 77, 512, 16
EPS = 1e-5


def silu(v):
    e = np.exp(-np.abs(v))
    return v * np.where(v >= 0.0, 1.0, e) / (1.0 + e)


def layer_norm(v, g, b):
    m = v.mean(-1, keepdims=True)
    var = ((v - m) ** 2).mean(-1, keepdims=True)
    return (v - m) / np.sqrt(var + EPS) * g + b


def setup_inputs():
    r = np.random.standard_normal
    s = mx_kscale(D)
    su = s / s.min()
    return {
        "x": bf(r((B, T, D))),
        "y": bf(r((B, T, D)) * 0.25),
        "emb0": bf(r((B, D)) * su),
        "We": bf(r((D, 2 * D)) / np.sqrt(D) / su[:, None]),
        "be": bf(r(2 * D) * 0.1),
        "ln2_g": bf(1.0 + 0.1 * r(D)),
        "ln2_b": bf(r(D) * 0.1),
        "Wo": bf(r((D, D)) / np.sqrt(D)),
        "bo": bf(r(D) * 0.1),
    }


def reference(x, y, emb0, We, be, ln2_g, ln2_b, Wo, bo):
    emb_out = (mxq(silu(f64(emb0)), 1, "e4m3") @ mxq(f64(We), 0, "e4m3")) + f64(be)
    scale, shift = emb_out[:, None, :D], emb_out[:, None, D:]
    h = layer_norm(f64(y), f64(ln2_g), f64(ln2_b)) * (1.0 + scale) + shift
    a = silu(h)
    return f64(x) + ((mxq(a, 2, "e4m3") @ mxq(f64(Wo), 0, "e4m3")) + f64(bo))

@@ -1,0 +1,295 @@
+from contextlib import ExitStack
+
+import concourse.mybir as mybir
+from concourse.masks import make_identity
+
+F32 = mybir.dt.float32
+BF16 = mybir.dt.bfloat16
+U32 = mybir.dt.uint32
+U8 = mybir.dt.uint8
+FP8X4 = mybir.dt.float8_e4m3fn_x4
+ACT = mybir.ActivationFunctionType
+ALU = mybir.AluOpType
+
+P = 128
+PACK = 4
+B, T, D = 128, 64, 512
+EPS = 1e-5
+
+ROWS = 4
+CHUNK = P * ROWS
+N_CHUNKS = B * T // CHUNK
+SEQS = CHUNK // T
+SEQ_PARTS = T // ROWS
+
+STATS_AHEAD = 3
+LOAD_AHEAD = STATS_AHEAD + 2
+
+GAIN_ROW, BETA_ROW, BE_ROW, BO_ROW, VEC_ROWS = 0, 4, 8, 16, 20
+
+FLOPS = 2 * B * T * D * D + 2 * B * D * 2 * D
+
+
+def interleave_k(copy, grouped, planes):
+    copy(
+        out=grouped.rearrange("p (c i) t -> p c t i", i=4),
+        in_=planes.rearrange("p t (c i) -> p c t i", i=4),
+    )
+
+
+def quantise(nc, codes, scales, grouped):
+    nc.vector.quantize_mx(
+        out=codes.bitcast(FP8X4),
+        scales=scales,
+        in_=grouped.rearrange("p w t -> p (w t)"),
+    )
+
+
+def tile_temporalcrossattention_pa_t_kernel(
+    tc, x, y, emb0, We, be, ln2_g, ln2_b, Wo, bo, out
+):
+    nc = tc.nc
+    x_chunks = x.flatten_outer_dims().rearrange("(c p j) d -> c p j d", p=P, j=ROWS)
+    y_chunks = y.flatten_outer_dims().rearrange("(c p j) d -> c p j d", p=P, j=ROWS)
+    out_chunks = out.flatten_outer_dims().rearrange("(c p j) d -> c p j d", p=P, j=ROWS)
+
+    with ExitStack() as ctx:
+        ctx.enter_context(tc.manual_schedule())
+        const = ctx.enter_context(tc.tile_pool(name="const", bufs=1))
+        y_pool = ctx.enter_context(tc.tile_pool(name="y", bufs=LOAD_AHEAD + 1))
+        x_pool = ctx.enter_context(tc.tile_pool(name="x", bufs=4))
+        stat_pool = ctx.enter_context(tc.tile_pool(name="stat", bufs=4))
+        norm_pool = ctx.enter_context(tc.tile_pool(name="norm", bufs=STATS_AHEAD))
+        work = ctx.enter_context(tc.tile_pool(name="work", bufs=2))
+        out_pool = ctx.enter_context(tc.tile_pool(name="out", bufs=3))
+        psum = ctx.enter_context(tc.psum_pool(name="psum", bufs=2))
+
+        y_tiles, x_tiles, norm_tiles, k_major_banks = {}, {}, {}, {}
+        act_tiles, grouped_tiles, code_tiles, product_tiles = {}, {}, {}, {}
+
+        def load_y(c):
+            y_sb = y_pool.tile([P, ROWS, D], BF16)
+            nc.sync.dma_start(out=y_sb[:], in_=y_chunks[c])
+            y_tiles[c] = y_sb
+
+        def load_x(c):
+            x_sb = x_pool.tile([P, ROWS, D], BF16)
+            nc.sync.dma_start(out=x_sb[:], in_=x_chunks[c])
+            x_tiles[c] = x_sb
+
+        def normalise(c):
+            y_sb = y_tiles[c]
+            stats = stat_pool.tile([P, ROWS, 6], F32)
+            mean_var = stat_pool.tile([P, ROWS, 2], F32)
+            for j in range(ROWS):
+                nc.vector.bn_stats(out=stats[:, j, :], in_=y_sb[:, j, :])
+            for j in range(ROWS):
+                nc.vector.bn_aggr(out=mean_var[:, j, :], in_=stats[:, j, :])
+            var_eps = stat_pool.tile([P, ROWS], F32)
+            neg_mean = stat_pool.tile([P, ROWS], F32)
+            rstd = stat_pool.tile([P, ROWS], F32)
+            nc.gpsimd.tensor_scalar(
+                out=var_eps[:], in0=mean_var[:, :, 1], scalar1=EPS, scalar2=1.0,
+                op0=ALU.add, op1=ALU.mult,
+            )
+            nc.gpsimd.tensor_scalar(
+                out=neg_mean[:], in0=mean_var[:, :, 0], scalar1=-1.0, scalar2=0.0,
+                op0=ALU.mult, op1=ALU.add,
+            )
+            nc.gpsimd.tensor_tensor(out=rstd[:], in0=var_eps[:], in1=minus_half[:], op=ALU.pow)
+            normed = norm_pool.tile([P, ROWS, D], F32)
+            for j in range(ROWS):
+                nc.gpsimd.tensor_scalar(
+                    out=normed[:, j, :], in0=y_sb[:, j, :],
+                    scalar1=neg_mean[:, j : j + 1], scalar2=rstd[:, j : j + 1],
+                    op0=ALU.add, op1=ALU.mult,
+                )
+            norm_tiles[c] = normed
+
+        def to_k_major(c):
+            normed = norm_tiles[c]
+            banks = []
+            for t in range(PACK):
+                k_major = psum.tile([P, ROWS, P], F32, bufs=PACK)
+                for j in range(ROWS):
+                    nc.tensor.transpose(
+                        out=k_major[:, j, :], in_=normed[:, j, t * P : (t + 1) * P],
+                        identity=ident_f32[:],
+                    )
+                banks.append(k_major)
+            k_major_banks[c] = banks
+
+        def modulate_silu(c):
+            acts = work.tile([P, PACK, ROWS, P], BF16)
+            for t in range(PACK):
+                k_major = k_major_banks[c][t]
+                for s in range(SEQS):
+                    b = c * SEQS + s
+                    frames = slice(s * SEQ_PARTS, (s + 1) * SEQ_PARTS)
+                    nc.scalar.activation(
+                        out=acts[:, t, :, frames], in_=k_major[:, :, frames], func=ACT.Silu,
+                        scale=mod_gain[:, t, b : b + 1], bias=mod_offset[:, t, b : b + 1],
+                    )
+            act_tiles[c] = acts
+
+        def regroup(c):
+            grouped = work.tile([P, CHUNK, PACK], BF16, align_bytes=64)
+            interleave_k(
+                nc.vector.tensor_copy, grouped[:],
+                act_tiles[c][:].rearrange("p t j q -> p t (j q)"),
+            )
+            grouped_tiles[c] = grouped
+
+        def quantise_acts(c):
+            act_codes = work.tile([P, CHUNK], U32, align_bytes=64)
+            act_scales = work.tile([P, CHUNK], U8, align_bytes=64)
+            quantise(nc, act_codes[:], act_scales[:], grouped_tiles[c][:])
+            code_tiles[c] = (act_codes, act_scales)
+
+        def project(c):
+            act_codes, act_scales = code_tiles[c]
+            product = work.tile([P, PACK, CHUNK], F32)
+            for m in range(PACK):
+                features = slice(m * P, (m + 1) * P)
+                acc = psum.tile([P, CHUNK], F32)
+                nc.tensor.matmul_mx(
+                    out=acc[:],
+                    lhsT=wo_codes[:, features].bitcast(FP8X4), lhsT_scale=wo_scales[:, features],
+                    rhs=act_codes[:].bitcast(FP8X4), rhs_scale=act_scales[:],
+                    start=True, stop=True,
+                )
+                nc.scalar.activation(
+                    out=product[:, m, :], in_=acc[:], func=ACT.Identity,
+                    bias=columns[:, BO_ROW + m : BO_ROW + m + 1],
+                )
+            product_tiles[c] = product
+
+        def add_residual_and_store(c):
+            product, x_sb = product_tiles[c], x_tiles[c]
+            result = out_pool.tile([P, ROWS, D], F32)
+            for j in range(ROWS):
+                token_major = psum.tile([P, PACK, P], F32)
+                for m in range(PACK):
+                    nc.tensor.transpose(
+                        out=token_major[:, m, :], in_=product[:, m, j * P : (j + 1) * P],
+                        identity=ident_f32[:],
+                    )
+                nc.vector.tensor_tensor(
+                    out=result[:, j, :], in0=token_major[:].rearrange("p m f -> p (m f)"),
+                    in1=x_sb[:, j, :], op=ALU.add,
+                )
+            nc.sync.dma_start(out=out_chunks[c], in_=result[:])
+
+        emb_sb = const.tile([P, D], BF16)
+        nc.sync.dma_start(out=emb_sb[:], in_=emb0)
+        vector_rows = const.tile([P, P], BF16)
+        nc.vector.memset(vector_rows[:], 0.0)
+        for first_row, vector in ((GAIN_ROW, ln2_g), (BETA_ROW, ln2_b), (BE_ROW, be), (BO_ROW, bo)):
+            rows = vector.rearrange("(r q) -> r q", q=P)
+            nc.sync.dma_start(out=vector_rows[first_row : first_row + rows.shape[0], :], in_=rows)
+        load_y(0)
+        we_planes = const.tile([P, PACK, 2 * D], BF16)
+        nc.sync.dma_start(out=we_planes[:], in_=We.rearrange("(t p) n -> p t n", p=P))
+        load_y(1)
+        wo_planes = const.tile([P, PACK, D], BF16)
+        nc.sync.dma_start(out=wo_planes[:], in_=Wo.rearrange("(t p) n -> p t n", p=P))
+        for c in range(2, LOAD_AHEAD):
+            load_y(c)
+
+        ident_bf16 = const.tile([P, P], BF16)
+        make_identity(nc, ident_bf16[:])
+        ident_f32 = const.tile([P, P], F32)
+        make_identity(nc, ident_f32[:])
+        minus_half = const.tile([P, ROWS], F32)
+        nc.gpsimd.memset(minus_half[:], -0.5)
+
+        emb_act = const.tile([P, D], BF16)
+        nc.scalar.activation(out=emb_act[:], in_=emb_sb[:], func=ACT.Silu)
+        emb_k_major = psum.tile([P, PACK, P], BF16, tag="token_major")
+        for t in range(PACK):
+            nc.tensor.transpose(
+                out=emb_k_major[:, t, :], in_=emb_act[:, t * P : (t + 1) * P], identity=ident_bf16[:]
+            )
+        emb_grouped = const.tile([P, B, PACK], BF16, align_bytes=64)
+        nc.vector.tensor_copy(out=emb_grouped[:], in_=emb_k_major[:].rearrange("p t b -> p b t"))
+        emb_codes = const.tile([P, B], U32, align_bytes=64)
+        emb_scales = const.tile([P, B], U8, align_bytes=64)
+
+        vector_columns = psum.tile([P, P], BF16, tag="token_major")
+        nc.tensor.transpose(out=vector_columns[:], in_=vector_rows[:], identity=ident_bf16[:])
+        columns = const.tile([P, VEC_ROWS], F32)
+        nc.vector.tensor_copy(out=columns[:], in_=vector_columns[:, 0:VEC_ROWS])
+        quantise(nc, emb_codes[:], emb_scales[:], emb_grouped[:])
+        gain = columns[:, GAIN_ROW : GAIN_ROW + PACK]
+        beta = columns[:, BETA_ROW : BETA_ROW + PACK]
+        be_scale = columns[:, BE_ROW : BE_ROW + PACK]
+        be_shift = columns[:, BE_ROW + PACK : BE_ROW + 2 * PACK]
+        one_plus_be = const.tile([P, PACK], F32)
+        gain_bias = const.tile([P, PACK], F32)
+        beta_bias = const.tile([P, PACK], F32)
+        offset_bias = const.tile([P, PACK], F32)
+        nc.vector.tensor_scalar_add(out=one_plus_be[:], in0=be_scale, scalar1=1.0)
+        nc.vector.tensor_mul(out=gain_bias[:], in0=gain, in1=one_plus_be[:])
+        nc.vector.tensor_mul(out=beta_bias[:], in0=beta, in1=one_plus_be[:])
+        nc.vector.tensor_add(out=offset_bias[:], in0=beta_bias[:], in1=be_shift)
+
+        normalise(0)
+
+        we_grouped = const.tile([P, 2 * D, PACK], BF16, align_bytes=64)
+        interleave_k(nc.vector.tensor_copy, we_grouped[:], we_planes[:])
+        wo_grouped = const.tile([P, D, PACK], BF16, align_bytes=64)
+        interleave_k(nc.scalar.copy, wo_grouped[:], wo_planes[:])
+        we_codes = const.tile([P, 2 * D], U32, align_bytes=64)
+        we_scales = const.tile([P, 2 * D], U8, align_bytes=64)
+        quantise(nc, we_codes[:], we_scales[:], we_grouped[:])
+        m_scale = psum.tile([P, PACK, B], F32, tag="acc")
+        m_shift = psum.tile([P, PACK, B], F32, tag="acc")
+        for half, sums in enumerate((m_scale, m_shift)):
+            for t in range(PACK):
+                features = slice((half * PACK + t) * P, (half * PACK + t + 1) * P)
+                nc.tensor.matmul_mx(
+                    out=sums[:, t, :],
+                    lhsT=we_codes[:, features].bitcast(FP8X4), lhsT_scale=we_scales[:, features],
+                    rhs=emb_codes[:].bitcast(FP8X4), rhs_scale=emb_scales[:],
+                    start=True, stop=True,
+                )
+        mod_gain = const.tile([P, PACK, B], F32)
+        offset_part = const.tile([P, PACK, B], F32)
+        mod_offset = const.tile([P, PACK, B], F32)
+        for t in range(PACK):
+            nc.scalar.activation(
+                out=offset_part[:, t, :], in_=m_scale[:, t, :], func=ACT.Identity,
+                scale=beta[:, t : t + 1], bias=offset_bias[:, t : t + 1],
+            )
+        for t in range(PACK):
+            nc.scalar.activation(
+                out=mod_gain[:, t, :], in_=m_scale[:, t, :], func=ACT.Identity,
+                scale=gain[:, t : t + 1], bias=gain_bias[:, t : t + 1],
+            )
+        normalise(1)
+        nc.vector.tensor_tensor(out=mod_offset[:], in0=m_shift[:], in1=offset_part[:], op=ALU.add)
+        wo_codes = const.tile([P, D], U32, align_bytes=64)
+        wo_scales = const.tile([P, D], U8, align_bytes=64)
+        quantise(nc, wo_codes[:], wo_scales[:], wo_grouped[:])
+        normalise(2)
+        to_k_major(0)
+
+        for c in range(N_CHUNKS + 2):
+            if c + LOAD_AHEAD < N_CHUNKS:
+                load_y(c + LOAD_AHEAD)
+            if c < N_CHUNKS:
+                load_x(c)
+            if 0 <= c - 1 < N_CHUNKS:
+                quantise_acts(c - 1)
+            if 0 <= c - 2:
+                add_residual_and_store(c - 2)
+            if c < N_CHUNKS:
+                modulate_silu(c)
+            if 0 <= c - 1 < N_CHUNKS:
+                project(c - 1)
+            if c < N_CHUNKS:
+                regroup(c)
+            if c + STATS_AHEAD < N_CHUNKS:
+                normalise(c + STATS_AHEAD)
+            if c + 1 < N_CHUNKS:
+                to_k_major(c + 1)

@@ -54,7 +54,6 @@ def tile_temporalcrossattention_pa_t_kernel(
     out_chunks = out.flatten_outer_dims().rearrange("(c p j) d -> c p j d", p=P, j=ROWS)
 
     with ExitStack() as ctx:
-        ctx.enter_context(tc.manual_schedule())
         const = ctx.enter_context(tc.tile_pool(name="const", bufs=1))
         y_pool = ctx.enter_context(tc.tile_pool(name="y", bufs=LOAD_AHEAD + 1))
         x_pool = ctx.enter_context(tc.tile_pool(name="x", bufs=4))

@@ -24,6 +24,7 @@ SEQ_PARTS = T // ROWS
 
 STATS_AHEAD = 3
 LOAD_AHEAD = STATS_AHEAD + 2
+PASS_ISSUES = 2
 
 GAIN_ROW, BETA_ROW, BE_ROW, BO_ROW, VEC_ROWS = 0, 4, 8, 16, 20
 
@@ -151,12 +152,14 @@ def tile_temporalcrossattention_pa_t_kernel(
             for m in range(PACK):
                 features = slice(m * P, (m + 1) * P)
                 acc = psum.tile([P, CHUNK], F32)
-                nc.tensor.matmul_mx(
-                    out=acc[:],
-                    lhsT=wo_codes[:, features].bitcast(FP8X4), lhsT_scale=wo_scales[:, features],
-                    rhs=act_codes[:].bitcast(FP8X4), rhs_scale=act_scales[:],
-                    start=True, stop=True,
-                )
+                for issue in range(PASS_ISSUES):
+                    nc.tensor.matmul_mx(
+                        out=acc[:],
+                        lhsT=wo_codes[:, features].bitcast(FP8X4),
+                        lhsT_scale=wo_scales[:, features],
+                        rhs=act_codes[:].bitcast(FP8X4), rhs_scale=act_scales[:],
+                        start=True, stop=True,
+                    )
                 nc.scalar.activation(
                     out=product[:, m, :], in_=acc[:], func=ACT.Identity,
                     bias=columns[:, BO_ROW + m : BO_ROW + m + 1],

@@ -22,9 +22,10 @@ N_CHUNKS = B * T // CHUNK
 SEQS = CHUNK // T
 SEQ_PARTS = T // ROWS
 
+VECTOR_TOKENS = 3 * P
+
 STATS_AHEAD = 3
 LOAD_AHEAD = STATS_AHEAD + 2
-PASS_ISSUES = 2
 
 GAIN_ROW, BETA_ROW, BE_ROW, BO_ROW, VEC_ROWS = 0, 4, 8, 16, 20
 
@@ -62,7 +63,7 @@ def tile_temporalcrossattention_pa_t_kernel(
         norm_pool = ctx.enter_context(tc.tile_pool(name="norm", bufs=STATS_AHEAD))
         work = ctx.enter_context(tc.tile_pool(name="work", bufs=2))
         out_pool = ctx.enter_context(tc.tile_pool(name="out", bufs=3))
-        psum = ctx.enter_context(tc.psum_pool(name="psum", bufs=2))
+        psum = ctx.enter_context(tc.psum_pool(name="psum", bufs=PACK))
 
         y_tiles, x_tiles, norm_tiles, k_major_banks = {}, {}, {}, {}
         act_tiles, grouped_tiles, code_tiles, product_tiles = {}, {}, {}, {}
@@ -110,7 +111,7 @@ def tile_temporalcrossattention_pa_t_kernel(
             normed = norm_tiles[c]
             banks = []
             for t in range(PACK):
-                k_major = psum.tile([P, ROWS, P], F32, bufs=PACK)
+                k_major = psum.tile([P, ROWS, P], F32)
                 for j in range(ROWS):
                     nc.tensor.transpose(
                         out=k_major[:, j, :], in_=normed[:, j, t * P : (t + 1) * P],
@@ -134,9 +135,12 @@ def tile_temporalcrossattention_pa_t_kernel(
 
         def regroup(c):
             grouped = work.tile([P, CHUNK, PACK], BF16, align_bytes=64)
+            planes = act_tiles[c][:].rearrange("p t j q -> p t (j q)")
             interleave_k(
-                nc.vector.tensor_copy, grouped[:],
-                act_tiles[c][:].rearrange("p t j q -> p t (j q)"),
+                nc.vector.tensor_copy, grouped[:, :VECTOR_TOKENS, :], planes[:, :, :VECTOR_TOKENS]
+            )
+            interleave_k(
+                nc.scalar.copy, grouped[:, VECTOR_TOKENS:, :], planes[:, :, VECTOR_TOKENS:]
             )
             grouped_tiles[c] = grouped
 
@@ -151,15 +155,13 @@ def tile_temporalcrossattention_pa_t_kernel(
             product = work.tile([P, PACK, CHUNK], F32)
             for m in range(PACK):
                 features = slice(m * P, (m + 1) * P)
-                acc = psum.tile([P, CHUNK], F32)
-                for issue in range(PASS_ISSUES):
-                    nc.tensor.matmul_mx(
-                        out=acc[:],
-                        lhsT=wo_codes[:, features].bitcast(FP8X4),
-                        lhsT_scale=wo_scales[:, features],
-                        rhs=act_codes[:].bitcast(FP8X4), rhs_scale=act_scales[:],
-                        start=True, stop=True,
-                    )
+                acc = psum.tile([P, CHUNK], F32, tag="ring")
+                nc.tensor.matmul_mx(
+                    out=acc[:],
+                    lhsT=wo_codes[:, features].bitcast(FP8X4), lhsT_scale=wo_scales[:, features],
+                    rhs=act_codes[:].bitcast(FP8X4), rhs_scale=act_scales[:],
+                    start=True, stop=True,
+                )
                 nc.scalar.activation(
                     out=product[:, m, :], in_=acc[:], func=ACT.Identity,
                     bias=columns[:, BO_ROW + m : BO_ROW + m + 1],
@@ -170,7 +172,7 @@ def tile_temporalcrossattention_pa_t_kernel(
             product, x_sb = product_tiles[c], x_tiles[c]
             result = out_pool.tile([P, ROWS, D], F32)
             for j in range(ROWS):
-                token_major = psum.tile([P, PACK, P], F32)
+                token_major = psum.tile([P, PACK, P], F32, tag="ring")
                 for m in range(PACK):
                     nc.tensor.transpose(
                         out=token_major[:, m, :], in_=product[:, m, j * P : (j + 1) * P],
@@ -180,7 +182,7 @@ def tile_temporalcrossattention_pa_t_kernel(
                     out=result[:, j, :], in0=token_major[:].rearrange("p m f -> p (m f)"),
                     in1=x_sb[:, j, :], op=ALU.add,
                 )
-            nc.sync.dma_start(out=out_chunks[c], in_=result[:])
+                nc.sync.dma_start(out=out_chunks[c][:, j, :], in_=result[:, j, :])
 
         emb_sb = const.tile([P, D], BF16)
         nc.sync.dma_start(out=emb_sb[:], in_=emb0)
@@ -207,7 +209,7 @@ def tile_temporalcrossattention_pa_t_kernel(
 
         emb_act = const.tile([P, D], BF16)
         nc.scalar.activation(out=emb_act[:], in_=emb_sb[:], func=ACT.Silu)
-        emb_k_major = psum.tile([P, PACK, P], BF16, tag="token_major")
+        emb_k_major = psum.tile([P, PACK, P], BF16, tag="ring")
         for t in range(PACK):
             nc.tensor.transpose(
                 out=emb_k_major[:, t, :], in_=emb_act[:, t * P : (t + 1) * P], identity=ident_bf16[:]
@@ -217,7 +219,7 @@ def tile_temporalcrossattention_pa_t_kernel(
         emb_codes = const.tile([P, B], U32, align_bytes=64)
         emb_scales = const.tile([P, B], U8, align_bytes=64)
 
-        vector_columns = psum.tile([P, P], BF16, tag="token_major")
+        vector_columns = psum.tile([P, P], BF16, tag="ring")
         nc.tensor.transpose(out=vector_columns[:], in_=vector_rows[:], identity=ident_bf16[:])
         columns = const.tile([P, VEC_ROWS], F32)
         nc.vector.tensor_copy(out=columns[:], in_=vector_columns[:, 0:VEC_ROWS])
@@ -238,15 +240,20 @@ def tile_temporalcrossattention_pa_t_kernel(
         normalise(0)
 
         we_grouped = const.tile([P, 2 * D, PACK], BF16, align_bytes=64)
-        interleave_k(nc.vector.tensor_copy, we_grouped[:], we_planes[:])
+        interleave_k(nc.vector.tensor_copy, we_grouped[:, :D, :], we_planes[:, :, :D])
+        interleave_k(nc.scalar.copy, we_grouped[:, D:, :], we_planes[:, :, D:])
         wo_grouped = const.tile([P, D, PACK], BF16, align_bytes=64)
         interleave_k(nc.scalar.copy, wo_grouped[:], wo_planes[:])
         we_codes = const.tile([P, 2 * D], U32, align_bytes=64)
         we_scales = const.tile([P, 2 * D], U8, align_bytes=64)
-        quantise(nc, we_codes[:], we_scales[:], we_grouped[:])
-        m_scale = psum.tile([P, PACK, B], F32, tag="acc")
-        m_shift = psum.tile([P, PACK, B], F32, tag="acc")
+        m_scale = psum.tile([P, PACK, B], F32, tag="ring")
+        m_shift = psum.tile([P, PACK, B], F32, tag="ring")
         for half, sums in enumerate((m_scale, m_shift)):
+            columns_of_half = slice(half * D, (half + 1) * D)
+            quantise(
+                nc, we_codes[:, columns_of_half], we_scales[:, columns_of_half],
+                we_grouped[:, columns_of_half, :],
+            )
             for t in range(PACK):
                 features = slice((half * PACK + t) * P, (half * PACK + t + 1) * P)
                 nc.tensor.matmul_mx(

@@ -24,8 +24,23 @@ SEQ_PARTS = T // ROWS
 
 VECTOR_TOKENS = 3 * P
 
-STATS_AHEAD = 3
-LOAD_AHEAD = STATS_AHEAD + 2
+STEPS = 4
+STATISTICS = -10
+NORMALISE = -5
+TO_K_MAJOR = 0
+MODULATE = 1
+REGROUP = 5
+QUANTISE = 6
+PROJECT = 7
+TO_TOKEN_MAJOR = 11
+ADD_RESIDUAL = 12
+LOAD_Y = -18
+LOAD_X = 4
+STATS_IN_PROLOGUE = 3
+Y_IN_PROLOGUE = 5
+PINNED = {
+    mybir.EngineType.PE, mybir.EngineType.DVE, mybir.EngineType.Activation, mybir.EngineType.Pool,
+}
 
 GAIN_ROW, BETA_ROW, BE_ROW, BO_ROW, VEC_ROWS = 0, 4, 8, 16, 20
 
@@ -57,16 +72,19 @@ def tile_temporalcrossattention_pa_t_kernel(
 
     with ExitStack() as ctx:
         const = ctx.enter_context(tc.tile_pool(name="const", bufs=1))
-        y_pool = ctx.enter_context(tc.tile_pool(name="y", bufs=LOAD_AHEAD + 1))
+        y_pool = ctx.enter_context(tc.tile_pool(name="y", bufs=6))
         x_pool = ctx.enter_context(tc.tile_pool(name="x", bufs=4))
         stat_pool = ctx.enter_context(tc.tile_pool(name="stat", bufs=4))
-        norm_pool = ctx.enter_context(tc.tile_pool(name="norm", bufs=STATS_AHEAD))
+        norm_pool = ctx.enter_context(tc.tile_pool(name="norm", bufs=3))
         work = ctx.enter_context(tc.tile_pool(name="work", bufs=2))
         out_pool = ctx.enter_context(tc.tile_pool(name="out", bufs=3))
+        product_pool = ctx.enter_context(tc.tile_pool(name="product", bufs=3))
         psum = ctx.enter_context(tc.psum_pool(name="psum", bufs=PACK))
+        ring = ctx.enter_context(tc.psum_pool(name="ring", bufs=2))
 
-        y_tiles, x_tiles, norm_tiles, k_major_banks = {}, {}, {}, {}
+        y_tiles, x_tiles, stat_tiles, norm_tiles, k_major_banks = {}, {}, {}, {}, {}
         act_tiles, grouped_tiles, code_tiles, product_tiles = {}, {}, {}, {}
+        token_major_banks, result_tiles = {}, {}
 
         def load_y(c):
             y_sb = y_pool.tile([P, ROWS, D], BF16)
@@ -78,14 +96,17 @@ def tile_temporalcrossattention_pa_t_kernel(
             nc.sync.dma_start(out=x_sb[:], in_=x_chunks[c])
             x_tiles[c] = x_sb
 
-        def normalise(c):
-            y_sb = y_tiles[c]
-            stats = stat_pool.tile([P, ROWS, 6], F32)
-            mean_var = stat_pool.tile([P, ROWS, 2], F32)
-            for j in range(ROWS):
-                nc.vector.bn_stats(out=stats[:, j, :], in_=y_sb[:, j, :])
-            for j in range(ROWS):
-                nc.vector.bn_aggr(out=mean_var[:, j, :], in_=stats[:, j, :])
+        def take_statistics(c, j):
+            if j == 0:
+                stats = stat_pool.tile([P, ROWS, 6], F32)
+                mean_var = stat_pool.tile([P, ROWS, 2], F32)
+                stat_tiles[c] = (stats, mean_var)
+            stats, mean_var = stat_tiles[c]
+            nc.vector.bn_stats(out=stats[:, j, :], in_=y_tiles[c][:, j, :])
+            if j < ROWS - 1:
+                return
+            for row in range(ROWS):
+                nc.vector.bn_aggr(out=mean_var[:, row, :], in_=stats[:, row, :])
             var_eps = stat_pool.tile([P, ROWS], F32)
             neg_mean = stat_pool.tile([P, ROWS], F32)
             rstd = stat_pool.tile([P, ROWS], F32)
@@ -98,40 +119,40 @@ def tile_temporalcrossattention_pa_t_kernel(
                 op0=ALU.mult, op1=ALU.add,
             )
             nc.gpsimd.tensor_tensor(out=rstd[:], in0=var_eps[:], in1=minus_half[:], op=ALU.pow)
-            normed = norm_pool.tile([P, ROWS, D], F32)
+            stat_tiles[c] = (neg_mean, rstd)
+
+        def normalise(c, j):
+            if j == 0:
+                normed = norm_pool.tile([P, ROWS, D], F32)
+                norm_tiles[c] = normed
+            neg_mean, rstd = stat_tiles[c]
+            nc.gpsimd.tensor_scalar(
+                out=norm_tiles[c][:, j, :], in0=y_tiles[c][:, j, :],
+                scalar1=neg_mean[:, j : j + 1], scalar2=rstd[:, j : j + 1],
+                op0=ALU.add, op1=ALU.mult,
+            )
+
+        def to_k_major(c, t):
+            k_major = psum.tile([P, ROWS, P], F32)
             for j in range(ROWS):
-                nc.gpsimd.tensor_scalar(
-                    out=normed[:, j, :], in0=y_sb[:, j, :],
-                    scalar1=neg_mean[:, j : j + 1], scalar2=rstd[:, j : j + 1],
-                    op0=ALU.add, op1=ALU.mult,
+                nc.tensor.transpose(
+                    out=k_major[:, j, :], in_=norm_tiles[c][:, j, t * P : (t + 1) * P],
+                    identity=ident_f32[:],
                 )
-            norm_tiles[c] = normed
+            k_major_banks[c, t] = k_major
 
-        def to_k_major(c):
-            normed = norm_tiles[c]
-            banks = []
-            for t in range(PACK):
-                k_major = psum.tile([P, ROWS, P], F32)
-                for j in range(ROWS):
-                    nc.tensor.transpose(
-                        out=k_major[:, j, :], in_=normed[:, j, t * P : (t + 1) * P],
-                        identity=ident_f32[:],
-                    )
-                banks.append(k_major)
-            k_major_banks[c] = banks
-
-        def modulate_silu(c):
-            acts = work.tile([P, PACK, ROWS, P], BF16)
-            for t in range(PACK):
-                k_major = k_major_banks[c][t]
-                for s in range(SEQS):
-                    b = c * SEQS + s
-                    frames = slice(s * SEQ_PARTS, (s + 1) * SEQ_PARTS)
-                    nc.scalar.activation(
-                        out=acts[:, t, :, frames], in_=k_major[:, :, frames], func=ACT.Silu,
-                        scale=mod_gain[:, t, b : b + 1], bias=mod_offset[:, t, b : b + 1],
-                    )
-            act_tiles[c] = acts
+        def modulate_silu(c, t):
+            if t == 0:
+                acts = work.tile([P, PACK, ROWS, P], BF16)
+                act_tiles[c] = acts
+            for s in range(SEQS):
+                b = c * SEQS + s
+                frames = slice(s * SEQ_PARTS, (s + 1) * SEQ_PARTS)
+                nc.scalar.activation(
+                    out=act_tiles[c][:, t, :, frames], in_=k_major_banks[c, t][:, :, frames],
+                    func=ACT.Silu,
+                    scale=mod_gain[:, t, b : b + 1], bias=mod_offset[:, t, b : b + 1],
+                )
 
         def regroup(c):
             grouped = work.tile([P, CHUNK, PACK], BF16, align_bytes=64)
@@ -150,39 +171,43 @@ def tile_temporalcrossattention_pa_t_kernel(
             quantise(nc, act_codes[:], act_scales[:], grouped_tiles[c][:])
             code_tiles[c] = (act_codes, act_scales)
 
-        def project(c):
+        def project(c, m):
+            if m == 0:
+                product = product_pool.tile([P, PACK, CHUNK], F32)
+                product_tiles[c] = product
             act_codes, act_scales = code_tiles[c]
-            product = work.tile([P, PACK, CHUNK], F32)
-            for m in range(PACK):
-                features = slice(m * P, (m + 1) * P)
-                acc = psum.tile([P, CHUNK], F32, tag="ring")
-                nc.tensor.matmul_mx(
-                    out=acc[:],
-                    lhsT=wo_codes[:, features].bitcast(FP8X4), lhsT_scale=wo_scales[:, features],
-                    rhs=act_codes[:].bitcast(FP8X4), rhs_scale=act_scales[:],
-                    start=True, stop=True,
-                )
-                nc.scalar.activation(
-                    out=product[:, m, :], in_=acc[:], func=ACT.Identity,
-                    bias=columns[:, BO_ROW + m : BO_ROW + m + 1],
-                )
-            product_tiles[c] = product
+            features = slice(m * P, (m + 1) * P)
+            acc = ring.tile([P, CHUNK], F32)
+            nc.tensor.matmul_mx(
+                out=acc[:],
+                lhsT=wo_codes[:, features].bitcast(FP8X4), lhsT_scale=wo_scales[:, features],
+                rhs=act_codes[:].bitcast(FP8X4), rhs_scale=act_scales[:],
+                start=True, stop=True,
+            )
+            nc.scalar.activation(
+                out=product_tiles[c][:, m, :], in_=acc[:], func=ACT.Identity,
+                bias=columns[:, BO_ROW + m : BO_ROW + m + 1],
+            )
 
-        def add_residual_and_store(c):
-            product, x_sb = product_tiles[c], x_tiles[c]
-            result = out_pool.tile([P, ROWS, D], F32)
-            for j in range(ROWS):
-                token_major = psum.tile([P, PACK, P], F32, tag="ring")
-                for m in range(PACK):
-                    nc.tensor.transpose(
-                        out=token_major[:, m, :], in_=product[:, m, j * P : (j + 1) * P],
-                        identity=ident_f32[:],
-                    )
-                nc.vector.tensor_tensor(
-                    out=result[:, j, :], in0=token_major[:].rearrange("p m f -> p (m f)"),
-                    in1=x_sb[:, j, :], op=ALU.add,
+        def to_token_major(c, j):
+            token_major = ring.tile([P, PACK, P], F32)
+            for m in range(PACK):
+                nc.tensor.transpose(
+                    out=token_major[:, m, :], in_=product_tiles[c][:, m, j * P : (j + 1) * P],
+                    identity=ident_f32[:],
                 )
-                nc.sync.dma_start(out=out_chunks[c][:, j, :], in_=result[:, j, :])
+            token_major_banks[c, j] = token_major
+
+        def add_residual_and_store(c, j):
+            if j == 0:
+                result = out_pool.tile([P, ROWS, D], F32)
+                result_tiles[c] = result
+            row = result_tiles[c][:, j, :]
+            nc.vector.tensor_tensor(
+                out=row, in0=token_major_banks[c, j][:].rearrange("p m f -> p (m f)"),
+                in1=x_tiles[c][:, j, :], op=ALU.add,
+            )
+            nc.sync.dma_start(out=out_chunks[c][:, j, :], in_=row)
 
         emb_sb = const.tile([P, D], BF16)
         nc.sync.dma_start(out=emb_sb[:], in_=emb0)
@@ -197,7 +222,7 @@ def tile_temporalcrossattention_pa_t_kernel(
         load_y(1)
         wo_planes = const.tile([P, PACK, D], BF16)
         nc.sync.dma_start(out=wo_planes[:], in_=Wo.rearrange("(t p) n -> p t n", p=P))
-        for c in range(2, LOAD_AHEAD):
+        for c in range(2, Y_IN_PROLOGUE):
             load_y(c)
 
         ident_bf16 = const.tile([P, P], BF16)
@@ -209,7 +234,7 @@ def tile_temporalcrossattention_pa_t_kernel(
 
         emb_act = const.tile([P, D], BF16)
         nc.scalar.activation(out=emb_act[:], in_=emb_sb[:], func=ACT.Silu)
-        emb_k_major = psum.tile([P, PACK, P], BF16, tag="ring")
+        emb_k_major = psum.tile([P, PACK, P], BF16, tag="k_major")
         for t in range(PACK):
             nc.tensor.transpose(
                 out=emb_k_major[:, t, :], in_=emb_act[:, t * P : (t + 1) * P], identity=ident_bf16[:]
@@ -219,7 +244,7 @@ def tile_temporalcrossattention_pa_t_kernel(
         emb_codes = const.tile([P, B], U32, align_bytes=64)
         emb_scales = const.tile([P, B], U8, align_bytes=64)
 
-        vector_columns = psum.tile([P, P], BF16, tag="ring")
+        vector_columns = psum.tile([P, P], BF16, tag="k_major")
         nc.tensor.transpose(out=vector_columns[:], in_=vector_rows[:], identity=ident_bf16[:])
         columns = const.tile([P, VEC_ROWS], F32)
         nc.vector.tensor_copy(out=columns[:], in_=vector_columns[:, 0:VEC_ROWS])
@@ -237,7 +262,10 @@ def tile_temporalcrossattention_pa_t_kernel(
         nc.vector.tensor_mul(out=beta_bias[:], in0=beta, in1=one_plus_be[:])
         nc.vector.tensor_add(out=offset_bias[:], in0=beta_bias[:], in1=be_shift)
 
-        normalise(0)
+        for j in range(ROWS):
+            take_statistics(0, j)
+        for j in range(ROWS):
+            normalise(0, j)
 
         we_grouped = const.tile([P, 2 * D, PACK], BF16, align_bytes=64)
         interleave_k(nc.vector.tensor_copy, we_grouped[:, :D, :], we_planes[:, :, :D])
@@ -246,8 +274,8 @@ def tile_temporalcrossattention_pa_t_kernel(
         interleave_k(nc.scalar.copy, wo_grouped[:], wo_planes[:])
         we_codes = const.tile([P, 2 * D], U32, align_bytes=64)
         we_scales = const.tile([P, 2 * D], U8, align_bytes=64)
-        m_scale = psum.tile([P, PACK, B], F32, tag="ring")
-        m_shift = psum.tile([P, PACK, B], F32, tag="ring")
+        m_scale = ring.tile([P, PACK, B], F32, tag="acc")
+        m_shift = ring.tile([P, PACK, B], F32, tag="acc")
         for half, sums in enumerate((m_scale, m_shift)):
             columns_of_half = slice(half * D, (half + 1) * D)
             quantise(
@@ -275,30 +303,37 @@ def tile_temporalcrossattention_pa_t_kernel(
                 out=mod_gain[:, t, :], in_=m_scale[:, t, :], func=ACT.Identity,
                 scale=gain[:, t : t + 1], bias=gain_bias[:, t : t + 1],
             )
-        normalise(1)
+        for j in range(ROWS):
+            take_statistics(1, j)
+        for j in range(ROWS):
+            normalise(1, j)
         nc.vector.tensor_tensor(out=mod_offset[:], in0=m_shift[:], in1=offset_part[:], op=ALU.add)
         wo_codes = const.tile([P, D], U32, align_bytes=64)
         wo_scales = const.tile([P, D], U8, align_bytes=64)
         quantise(nc, wo_codes[:], wo_scales[:], wo_grouped[:])
-        normalise(2)
-        to_k_major(0)
+        for j in range(ROWS):
+            take_statistics(2, j)
 
-        for c in range(N_CHUNKS + 2):
-            if c + LOAD_AHEAD < N_CHUNKS:
-                load_y(c + LOAD_AHEAD)
-            if c < N_CHUNKS:
-                load_x(c)
-            if 0 <= c - 1 < N_CHUNKS:
-                quantise_acts(c - 1)
-            if 0 <= c - 2:
-                add_residual_and_store(c - 2)
-            if c < N_CHUNKS:
-                modulate_silu(c)
-            if 0 <= c - 1 < N_CHUNKS:
-                project(c - 1)
-            if c < N_CHUNKS:
-                regroup(c)
-            if c + STATS_AHEAD < N_CHUNKS:
-                normalise(c + STATS_AHEAD)
-            if c + 1 < N_CHUNKS:
-                to_k_major(c + 1)
+        def in_step(step, begin, stage, first_chunk=0):
+            c, part = divmod(step - begin, STEPS)
+            if first_chunk <= c < N_CHUNKS:
+                stage(c, part)
+
+        def at_step(step, begin, stage, first_chunk=0):
+            c, part = divmod(step - begin, STEPS)
+            if part == 0 and first_chunk <= c < N_CHUNKS:
+                stage(c)
+
+        with tc.manual_schedule(engines=PINNED):
+            for step in range(STEPS * (N_CHUNKS - 1) + ADD_RESIDUAL + STEPS):
+                at_step(step, LOAD_Y, load_y, Y_IN_PROLOGUE)
+                at_step(step, LOAD_X, load_x)
+                in_step(step, ADD_RESIDUAL, add_residual_and_store)
+                in_step(step, MODULATE, modulate_silu)
+                at_step(step, REGROUP, regroup)
+                at_step(step, QUANTISE, quantise_acts)
+                in_step(step, PROJECT, project)
+                in_step(step, TO_K_MAJOR, to_k_major)
+                in_step(step, TO_TOKEN_MAJOR, to_token_major)
+                in_step(step, STATISTICS, take_statistics, STATS_IN_PROLOGUE)
+                in_step(step, NORMALISE, normalise, STATS_IN_PROLOGUE - 1)

@@ -134,6 +134,12 @@ def tile_temporalcrossattention_pa_t_kernel(
 
         def to_k_major(c, t):
             k_major = psum.tile([P, ROWS, P], F32)
+            nc.tensor.matmul_mx(
+                out=k_major[:].rearrange("p j q -> p (j q)"),
+                lhsT=wo_codes[:, 0:P].bitcast(FP8X4), lhsT_scale=wo_scales[:, 0:P],
+                rhs=wo_codes[:].bitcast(FP8X4), rhs_scale=wo_scales[:],
+                start=True, stop=True,
+            )
             for j in range(ROWS):
                 nc.tensor.transpose(
                     out=k_major[:, j, :], in_=norm_tiles[c][:, j, t * P : (t + 1) * P],

@@ -25,12 +25,12 @@ SEQ_PARTS = T // ROWS
 VECTOR_TOKENS = 3 * P
 
 STEPS = 4
-STATISTICS = -10
-NORMALISE = -5
+STATISTICS = -11
+NORMALISE = -6
 TO_K_MAJOR = 0
 MODULATE = 1
 REGROUP = 5
-QUANTISE = 6
+QUANTISE = 5
 PROJECT = 7
 TO_TOKEN_MAJOR = 11
 ADD_RESIDUAL = 12
@@ -136,8 +136,8 @@ def tile_temporalcrossattention_pa_t_kernel(
             k_major = psum.tile([P, ROWS, P], F32)
             nc.tensor.matmul_mx(
                 out=k_major[:].rearrange("p j q -> p (j q)"),
-                lhsT=wo_codes[:, 0:P].bitcast(FP8X4), lhsT_scale=wo_scales[:, 0:P],
-                rhs=wo_codes[:].bitcast(FP8X4), rhs_scale=wo_scales[:],
+                lhsT=we_codes[:, 0:P].bitcast(FP8X4), lhsT_scale=we_scales[:, 0:P],
+                rhs=we_codes[:, 0:CHUNK].bitcast(FP8X4), rhs_scale=we_scales[:, 0:CHUNK],
                 start=True, stop=True,
             )
             for j in range(ROWS):
@@ -337,9 +337,9 @@ def tile_temporalcrossattention_pa_t_kernel(
                 in_step(step, ADD_RESIDUAL, add_residual_and_store)
                 in_step(step, MODULATE, modulate_silu)
                 at_step(step, REGROUP, regroup)
-                at_step(step, QUANTISE, quantise_acts)
                 in_step(step, PROJECT, project)
                 in_step(step, TO_K_MAJOR, to_k_major)
                 in_step(step, TO_TOKEN_MAJOR, to_token_major)
                 in_step(step, STATISTICS, take_statistics, STATS_IN_PROLOGUE)
+                at_step(step, QUANTISE, quantise_acts)
                 in_step(step, NORMALISE, normalise, STATS_IN_PROLOGUE - 1)

@@ -25,7 +25,8 @@ SEQ_PARTS = T // ROWS
 VECTOR_TOKENS = 3 * P
 
 STEPS = 4
-STATISTICS = -11
+STATISTICS = -12
+FINISH_STATISTICS = -8
 NORMALISE = -6
 TO_K_MAJOR = 0
 MODULATE = 1
@@ -82,7 +83,7 @@ def tile_temporalcrossattention_pa_t_kernel(
         psum = ctx.enter_context(tc.psum_pool(name="psum", bufs=PACK))
         ring = ctx.enter_context(tc.psum_pool(name="ring", bufs=2))
 
-        y_tiles, x_tiles, stat_tiles, norm_tiles, k_major_banks = {}, {}, {}, {}, {}
+        y_tiles, x_tiles, stat_tiles, moment_tiles, norm_tiles, k_major_banks = {}, {}, {}, {}, {}, {}
         act_tiles, grouped_tiles, code_tiles, product_tiles = {}, {}, {}, {}
         token_major_banks, result_tiles = {}, {}
 
@@ -98,34 +99,27 @@ def tile_temporalcrossattention_pa_t_kernel(
 
         def take_statistics(c, j):
             if j == 0:
-                stats = stat_pool.tile([P, ROWS, 6], F32)
                 mean_var = stat_pool.tile([P, ROWS, 2], F32)
-                stat_tiles[c] = (stats, mean_var)
-            stats, mean_var = stat_tiles[c]
-            nc.vector.bn_stats(out=stats[:, j, :], in_=y_tiles[c][:, j, :])
-            if j < ROWS - 1:
-                return
-            for row in range(ROWS):
-                nc.vector.bn_aggr(out=mean_var[:, row, :], in_=stats[:, row, :])
+                stat_tiles[c] = mean_var
+            stats = stat_pool.tile([P, 6], F32)
+            nc.vector.bn_stats(out=stats[:], in_=y_tiles[c][:, j, :])
+            nc.vector.bn_aggr(out=stat_tiles[c][:, j, :], in_=stats[:])
+
+        def finish_statistics(c):
+            mean_var = stat_tiles[c]
             var_eps = stat_pool.tile([P, ROWS], F32)
             neg_mean = stat_pool.tile([P, ROWS], F32)
             rstd = stat_pool.tile([P, ROWS], F32)
-            nc.gpsimd.tensor_scalar(
-                out=var_eps[:], in0=mean_var[:, :, 1], scalar1=EPS, scalar2=1.0,
-                op0=ALU.add, op1=ALU.mult,
-            )
-            nc.gpsimd.tensor_scalar(
-                out=neg_mean[:], in0=mean_var[:, :, 0], scalar1=-1.0, scalar2=0.0,
-                op0=ALU.mult, op1=ALU.add,
-            )
+            nc.vector.tensor_scalar_add(out=var_eps[:], in0=mean_var[:, :, 1], scalar1=EPS)
+            nc.vector.tensor_scalar_mul(out=neg_mean[:], in0=mean_var[:, :, 0], scalar1=-1.0)
             nc.gpsimd.tensor_tensor(out=rstd[:], in0=var_eps[:], in1=minus_half[:], op=ALU.pow)
-            stat_tiles[c] = (neg_mean, rstd)
+            moment_tiles[c] = (neg_mean, rstd)
 
         def normalise(c, j):
             if j == 0:
                 normed = norm_pool.tile([P, ROWS, D], F32)
                 norm_tiles[c] = normed
-            neg_mean, rstd = stat_tiles[c]
+            neg_mean, rstd = moment_tiles[c]
             nc.gpsimd.tensor_scalar(
                 out=norm_tiles[c][:, j, :], in0=y_tiles[c][:, j, :],
                 scalar1=neg_mean[:, j : j + 1], scalar2=rstd[:, j : j + 1],
@@ -270,6 +264,7 @@ def tile_temporalcrossattention_pa_t_kernel(
 
         for j in range(ROWS):
             take_statistics(0, j)
+        finish_statistics(0)
         for j in range(ROWS):
             normalise(0, j)
 
@@ -311,6 +306,7 @@ def tile_temporalcrossattention_pa_t_kernel(
             )
         for j in range(ROWS):
             take_statistics(1, j)
+        finish_statistics(1)
         for j in range(ROWS):
             normalise(1, j)
         nc.vector.tensor_tensor(out=mod_offset[:], in0=m_shift[:], in1=offset_part[:], op=ALU.add)
@@ -319,6 +315,7 @@ def tile_temporalcrossattention_pa_t_kernel(
         quantise(nc, wo_codes[:], wo_scales[:], wo_grouped[:])
         for j in range(ROWS):
             take_statistics(2, j)
+        finish_statistics(2)
 
         def in_step(step, begin, stage, first_chunk=0):
             c, part = divmod(step - begin, STEPS)
@@ -343,3 +340,4 @@ def tile_temporalcrossattention_pa_t_kernel(
                 in_step(step, STATISTICS, take_statistics, STATS_IN_PROLOGUE)
                 at_step(step, QUANTISE, quantise_acts)
                 in_step(step, NORMALISE, normalise, STATS_IN_PROLOGUE - 1)
+                at_step(step, FINISH_STATISTICS, finish_statistics, STATS_IN_PROLOGUE)

@@ -26,6 +26,7 @@ VECTOR_TOKENS = 3 * P
 
 STEPS = 4
 STATISTICS = -12
+AGGREGATE = -11
 FINISH_STATISTICS = -8
 NORMALISE = -6
 TO_K_MAJOR = 0
@@ -99,14 +100,17 @@ def tile_temporalcrossattention_pa_t_kernel(
 
         def take_statistics(c, j):
             if j == 0:
+                stats = stat_pool.tile([P, ROWS, 6], F32)
                 mean_var = stat_pool.tile([P, ROWS, 2], F32)
-                stat_tiles[c] = mean_var
-            stats = stat_pool.tile([P, 6], F32)
-            nc.vector.bn_stats(out=stats[:], in_=y_tiles[c][:, j, :])
-            nc.vector.bn_aggr(out=stat_tiles[c][:, j, :], in_=stats[:])
+                stat_tiles[c] = (stats, mean_var)
+            nc.vector.bn_stats(out=stat_tiles[c][0][:, j, :], in_=y_tiles[c][:, j, :])
+
+        def aggregate(c, j):
+            stats, mean_var = stat_tiles[c]
+            nc.vector.bn_aggr(out=mean_var[:, j, :], in_=stats[:, j, :])
 
         def finish_statistics(c):
-            mean_var = stat_tiles[c]
+            mean_var = stat_tiles[c][1]
             var_eps = stat_pool.tile([P, ROWS], F32)
             neg_mean = stat_pool.tile([P, ROWS], F32)
             rstd = stat_pool.tile([P, ROWS], F32)
@@ -264,6 +268,8 @@ def tile_temporalcrossattention_pa_t_kernel(
 
         for j in range(ROWS):
             take_statistics(0, j)
+        for j in range(ROWS):
+            aggregate(0, j)
         finish_statistics(0)
         for j in range(ROWS):
             normalise(0, j)
@@ -306,6 +312,8 @@ def tile_temporalcrossattention_pa_t_kernel(
             )
         for j in range(ROWS):
             take_statistics(1, j)
+        for j in range(ROWS):
+            aggregate(1, j)
         finish_statistics(1)
         for j in range(ROWS):
             normalise(1, j)
@@ -315,6 +323,8 @@ def tile_temporalcrossattention_pa_t_kernel(
         quantise(nc, wo_codes[:], wo_scales[:], wo_grouped[:])
         for j in range(ROWS):
             take_statistics(2, j)
+        for j in range(ROWS):
+            aggregate(2, j)
         finish_statistics(2)
 
         def in_step(step, begin, stage, first_chunk=0):
@@ -337,6 +347,7 @@ def tile_temporalcrossattention_pa_t_kernel(
                 in_step(step, PROJECT, project)
                 in_step(step, TO_K_MAJOR, to_k_major)
                 in_step(step, TO_TOKEN_MAJOR, to_token_major)
+                in_step(step, AGGREGATE, aggregate, STATS_IN_PROLOGUE)
                 in_step(step, STATISTICS, take_statistics, STATS_IN_PROLOGUE)
                 at_step(step, QUANTISE, quantise_acts)
                 in_step(step, NORMALISE, normalise, STATS_IN_PROLOGUE - 1)

@@ -25,8 +25,8 @@ SEQ_PARTS = T // ROWS
 VECTOR_TOKENS = 3 * P
 
 STEPS = 4
-STATISTICS = -12
-AGGREGATE = -11
+STATISTICS = -13
+AGGREGATE = -12
 FINISH_STATISTICS = -8
 NORMALISE = -6
 TO_K_MAJOR = 0
@@ -37,8 +37,16 @@ PROJECT = 7
 TO_TOKEN_MAJOR = 11
 ADD_RESIDUAL = 12
 LOAD_Y = -18
-LOAD_X = 4
-STATS_IN_PROLOGUE = 3
+LOAD_X = 0
+DIRECT_FROM = N_CHUNKS - 3
+ADD_BIAS = 5
+ADD_RESIDUAL_DIRECT = 8
+LOAD_BO = 32
+TENSOR_ROWS = (0,)
+WARM_BLOCKS = (0, 2)
+STATS_IN_PROLOGUE = 4
+MOMENTS_IN_PROLOGUE = 4
+NORM_IN_PROLOGUE = 2
 Y_IN_PROLOGUE = 5
 PINNED = {
     mybir.EngineType.PE, mybir.EngineType.DVE, mybir.EngineType.Activation, mybir.EngineType.Pool,
@@ -75,18 +83,19 @@ def tile_temporalcrossattention_pa_t_kernel(
     with ExitStack() as ctx:
         const = ctx.enter_context(tc.tile_pool(name="const", bufs=1))
         y_pool = ctx.enter_context(tc.tile_pool(name="y", bufs=6))
-        x_pool = ctx.enter_context(tc.tile_pool(name="x", bufs=4))
+        x_pool = ctx.enter_context(tc.tile_pool(name="x", bufs=7))
         stat_pool = ctx.enter_context(tc.tile_pool(name="stat", bufs=4))
         norm_pool = ctx.enter_context(tc.tile_pool(name="norm", bufs=3))
         work = ctx.enter_context(tc.tile_pool(name="work", bufs=2))
-        out_pool = ctx.enter_context(tc.tile_pool(name="out", bufs=3))
+        xb_pool = ctx.enter_context(tc.tile_pool(name="xb", bufs=3))
+        out_pool = ctx.enter_context(tc.tile_pool(name="out", bufs=4))
         product_pool = ctx.enter_context(tc.tile_pool(name="product", bufs=3))
         psum = ctx.enter_context(tc.psum_pool(name="psum", bufs=PACK))
         ring = ctx.enter_context(tc.psum_pool(name="ring", bufs=2))
 
         y_tiles, x_tiles, stat_tiles, moment_tiles, norm_tiles, k_major_banks = {}, {}, {}, {}, {}, {}
         act_tiles, grouped_tiles, code_tiles, product_tiles = {}, {}, {}, {}
-        token_major_banks, result_tiles = {}, {}
+        token_major_banks, result_tiles, residual_tiles = {}, {}, {}
 
         def load_y(c):
             y_sb = y_pool.tile([P, ROWS, D], BF16)
@@ -109,35 +118,49 @@ def tile_temporalcrossattention_pa_t_kernel(
             stats, mean_var = stat_tiles[c]
             nc.vector.bn_aggr(out=mean_var[:, j, :], in_=stats[:, j, :])
 
-        def finish_statistics(c):
+        def finish_statistics(c, on_vector=False):
             mean_var = stat_tiles[c][1]
             var_eps = stat_pool.tile([P, ROWS], F32)
             neg_mean = stat_pool.tile([P, ROWS], F32)
             rstd = stat_pool.tile([P, ROWS], F32)
-            nc.vector.tensor_scalar_add(out=var_eps[:], in0=mean_var[:, :, 1], scalar1=EPS)
-            nc.vector.tensor_scalar_mul(out=neg_mean[:], in0=mean_var[:, :, 0], scalar1=-1.0)
+            mean, var = mean_var[:, :, 0], mean_var[:, :, 1]
+            if on_vector:
+                nc.vector.tensor_scalar_add(out=var_eps[:], in0=var, scalar1=EPS)
+                nc.vector.tensor_scalar_mul(out=neg_mean[:], in0=mean, scalar1=-1.0)
+            else:
+                nc.scalar.activation(out=var_eps[:], in_=var, func=ACT.Identity, bias=EPS)
+                nc.scalar.activation(out=neg_mean[:], in_=mean, func=ACT.Copy, scale=-1.0)
             nc.gpsimd.tensor_tensor(out=rstd[:], in0=var_eps[:], in1=minus_half[:], op=ALU.pow)
             moment_tiles[c] = (neg_mean, rstd)
 
-        def normalise(c, j):
+        def normalise(c, j, engine=nc.gpsimd):
             if j == 0:
                 normed = norm_pool.tile([P, ROWS, D], F32)
                 norm_tiles[c] = normed
             neg_mean, rstd = moment_tiles[c]
-            nc.gpsimd.tensor_scalar(
+            engine.tensor_scalar(
                 out=norm_tiles[c][:, j, :], in0=y_tiles[c][:, j, :],
                 scalar1=neg_mean[:, j : j + 1], scalar2=rstd[:, j : j + 1],
                 op0=ALU.add, op1=ALU.mult,
             )
 
+        def add_bias(c, j):
+            if j == 0:
+                residual = xb_pool.tile([P, ROWS, D], F32)
+                residual_tiles[c] = residual
+            nc.gpsimd.tensor_tensor(
+                out=residual_tiles[c][:, j, :], in0=x_tiles[c][:, j, :], in1=bo_rows[:], op=ALU.add
+            )
+
         def to_k_major(c, t):
             k_major = psum.tile([P, ROWS, P], F32)
-            nc.tensor.matmul_mx(
-                out=k_major[:].rearrange("p j q -> p (j q)"),
-                lhsT=we_codes[:, 0:P].bitcast(FP8X4), lhsT_scale=we_scales[:, 0:P],
-                rhs=we_codes[:, 0:CHUNK].bitcast(FP8X4), rhs_scale=we_scales[:, 0:CHUNK],
-                start=True, stop=True,
-            )
+            if t in WARM_BLOCKS:
+                nc.tensor.matmul_mx(
+                    out=k_major[:].rearrange("p j q -> p (j q)"),
+                    lhsT=we_codes[:, 0:P].bitcast(FP8X4), lhsT_scale=we_scales[:, 0:P],
+                    rhs=we_codes[:, 0:CHUNK].bitcast(FP8X4), rhs_scale=we_scales[:, 0:CHUNK],
+                    start=True, stop=True,
+                )
             for j in range(ROWS):
                 nc.tensor.transpose(
                     out=k_major[:, j, :], in_=norm_tiles[c][:, j, t * P : (t + 1) * P],
@@ -193,13 +216,35 @@ def tile_temporalcrossattention_pa_t_kernel(
                 bias=columns[:, BO_ROW + m : BO_ROW + m + 1],
             )
 
+        def project_direct(c, j):
+            act_codes, act_scales = code_tiles[c]
+            tokens = slice(j * P, (j + 1) * P)
+            acc = ring.tile([P, D], F32)
+            nc.tensor.matmul_mx(
+                out=acc[:],
+                lhsT=act_codes[:, tokens].bitcast(FP8X4), lhsT_scale=act_scales[:, tokens],
+                rhs=wo_codes[:].bitcast(FP8X4), rhs_scale=wo_scales[:],
+                start=True, stop=True,
+            )
+            token_major_banks[c, j] = acc
+
         def to_token_major(c, j):
-            token_major = ring.tile([P, PACK, P], F32)
-            for m in range(PACK):
-                nc.tensor.transpose(
-                    out=token_major[:, m, :], in_=product_tiles[c][:, m, j * P : (j + 1) * P],
-                    identity=ident_f32[:],
+            token_major = ring.tile([P, D], F32)
+            if j in TENSOR_ROWS:
+                nc.tensor.matmul(
+                    out=token_major[:], lhsT=ident_bf16[:], rhs=x_tiles[c][:, j, :],
+                    start=True, stop=False,
                 )
+            for m in range(PACK):
+                columns_of_block = token_major[:, m * P : (m + 1) * P]
+                block = product_tiles[c][:, m, j * P : (j + 1) * P]
+                if j in TENSOR_ROWS:
+                    nc.tensor.matmul(
+                        out=columns_of_block, lhsT=block, rhs=ident_f32[:], is_transpose=True,
+                        start=False, stop=m == PACK - 1,
+                    )
+                else:
+                    nc.tensor.transpose(out=columns_of_block, in_=block, identity=ident_f32[:])
             token_major_banks[c, j] = token_major
 
         def add_residual_and_store(c, j):
@@ -207,10 +252,13 @@ def tile_temporalcrossattention_pa_t_kernel(
                 result = out_pool.tile([P, ROWS, D], F32)
                 result_tiles[c] = result
             row = result_tiles[c][:, j, :]
-            nc.vector.tensor_tensor(
-                out=row, in0=token_major_banks[c, j][:].rearrange("p m f -> p (m f)"),
-                in1=x_tiles[c][:, j, :], op=ALU.add,
-            )
+            if c < DIRECT_FROM and j in TENSOR_ROWS:
+                nc.scalar.copy(out=row, in_=token_major_banks[c, j][:])
+            else:
+                residual = residual_tiles[c] if c >= DIRECT_FROM else x_tiles[c]
+                nc.vector.tensor_tensor(
+                    out=row, in0=token_major_banks[c, j][:], in1=residual[:, j, :], op=ALU.add
+                )
             nc.sync.dma_start(out=out_chunks[c][:, j, :], in_=row)
 
         emb_sb = const.tile([P, D], BF16)
@@ -237,22 +285,10 @@ def tile_temporalcrossattention_pa_t_kernel(
         nc.gpsimd.memset(minus_half[:], -0.5)
 
         emb_act = const.tile([P, D], BF16)
-        nc.scalar.activation(out=emb_act[:], in_=emb_sb[:], func=ACT.Silu)
-        emb_k_major = psum.tile([P, PACK, P], BF16, tag="k_major")
-        for t in range(PACK):
-            nc.tensor.transpose(
-                out=emb_k_major[:, t, :], in_=emb_act[:, t * P : (t + 1) * P], identity=ident_bf16[:]
-            )
         emb_grouped = const.tile([P, B, PACK], BF16, align_bytes=64)
-        nc.vector.tensor_copy(out=emb_grouped[:], in_=emb_k_major[:].rearrange("p t b -> p b t"))
         emb_codes = const.tile([P, B], U32, align_bytes=64)
         emb_scales = const.tile([P, B], U8, align_bytes=64)
-
-        vector_columns = psum.tile([P, P], BF16, tag="k_major")
-        nc.tensor.transpose(out=vector_columns[:], in_=vector_rows[:], identity=ident_bf16[:])
         columns = const.tile([P, VEC_ROWS], F32)
-        nc.vector.tensor_copy(out=columns[:], in_=vector_columns[:, 0:VEC_ROWS])
-        quantise(nc, emb_codes[:], emb_scales[:], emb_grouped[:])
         gain = columns[:, GAIN_ROW : GAIN_ROW + PACK]
         beta = columns[:, BETA_ROW : BETA_ROW + PACK]
         be_scale = columns[:, BE_ROW : BE_ROW + PACK]
@@ -261,29 +297,20 @@ def tile_temporalcrossattention_pa_t_kernel(
         gain_bias = const.tile([P, PACK], F32)
         beta_bias = const.tile([P, PACK], F32)
         offset_bias = const.tile([P, PACK], F32)
-        nc.vector.tensor_scalar_add(out=one_plus_be[:], in0=be_scale, scalar1=1.0)
-        nc.vector.tensor_mul(out=gain_bias[:], in0=gain, in1=one_plus_be[:])
-        nc.vector.tensor_mul(out=beta_bias[:], in0=beta, in1=one_plus_be[:])
-        nc.vector.tensor_add(out=offset_bias[:], in0=beta_bias[:], in1=be_shift)
-
-        for j in range(ROWS):
-            take_statistics(0, j)
-        for j in range(ROWS):
-            aggregate(0, j)
-        finish_statistics(0)
-        for j in range(ROWS):
-            normalise(0, j)
-
         we_grouped = const.tile([P, 2 * D, PACK], BF16, align_bytes=64)
-        interleave_k(nc.vector.tensor_copy, we_grouped[:, :D, :], we_planes[:, :, :D])
-        interleave_k(nc.scalar.copy, we_grouped[:, D:, :], we_planes[:, :, D:])
-        wo_grouped = const.tile([P, D, PACK], BF16, align_bytes=64)
-        interleave_k(nc.scalar.copy, wo_grouped[:], wo_planes[:])
         we_codes = const.tile([P, 2 * D], U32, align_bytes=64)
         we_scales = const.tile([P, 2 * D], U8, align_bytes=64)
+        wo_grouped = const.tile([P, D, PACK], BF16, align_bytes=64)
+        wo_codes = const.tile([P, D], U32, align_bytes=64)
+        wo_scales = const.tile([P, D], U8, align_bytes=64)
         m_scale = ring.tile([P, PACK, B], F32, tag="acc")
         m_shift = ring.tile([P, PACK, B], F32, tag="acc")
-        for half, sums in enumerate((m_scale, m_shift)):
+        mod_gain = const.tile([P, PACK, B], F32)
+        offset_part = const.tile([P, PACK, B], F32)
+        mod_offset = const.tile([P, PACK, B], F32)
+        bo_rows = const.tile([P, D], BF16)
+
+        def embed(half, sums):
             columns_of_half = slice(half * D, (half + 1) * D)
             quantise(
                 nc, we_codes[:, columns_of_half], we_scales[:, columns_of_half],
@@ -297,58 +324,105 @@ def tile_temporalcrossattention_pa_t_kernel(
                     rhs=emb_codes[:].bitcast(FP8X4), rhs_scale=emb_scales[:],
                     start=True, stop=True,
                 )
-        mod_gain = const.tile([P, PACK, B], F32)
-        offset_part = const.tile([P, PACK, B], F32)
-        mod_offset = const.tile([P, PACK, B], F32)
-        for t in range(PACK):
-            nc.scalar.activation(
-                out=offset_part[:, t, :], in_=m_scale[:, t, :], func=ACT.Identity,
-                scale=beta[:, t : t + 1], bias=offset_bias[:, t : t + 1],
-            )
-        for t in range(PACK):
-            nc.scalar.activation(
-                out=mod_gain[:, t, :], in_=m_scale[:, t, :], func=ACT.Identity,
-                scale=gain[:, t : t + 1], bias=gain_bias[:, t : t + 1],
-            )
-        for j in range(ROWS):
-            take_statistics(1, j)
-        for j in range(ROWS):
-            aggregate(1, j)
-        finish_statistics(1)
-        for j in range(ROWS):
-            normalise(1, j)
-        nc.vector.tensor_tensor(out=mod_offset[:], in0=m_shift[:], in1=offset_part[:], op=ALU.add)
-        wo_codes = const.tile([P, D], U32, align_bytes=64)
-        wo_scales = const.tile([P, D], U8, align_bytes=64)
-        quantise(nc, wo_codes[:], wo_scales[:], wo_grouped[:])
-        for j in range(ROWS):
-            take_statistics(2, j)
-        for j in range(ROWS):
-            aggregate(2, j)
-        finish_statistics(2)
 
-        def in_step(step, begin, stage, first_chunk=0):
+        with tc.manual_schedule(engines=PINNED):
+            nc.scalar.activation(out=emb_act[:], in_=emb_sb[:], func=ACT.Silu)
+            emb_k_major = psum.tile([P, PACK, P], BF16, tag="k_major")
+            for t in range(PACK):
+                nc.tensor.transpose(
+                    out=emb_k_major[:, t, :], in_=emb_act[:, t * P : (t + 1) * P],
+                    identity=ident_bf16[:],
+                )
+            vector_columns = psum.tile([P, P], BF16, tag="k_major")
+            nc.tensor.transpose(
+                out=vector_columns[:], in_=vector_rows[:], identity=ident_bf16[:]
+            )
+            nc.vector.tensor_copy(
+                out=emb_grouped[:], in_=emb_k_major[:].rearrange("p t b -> p b t")
+            )
+            take_statistics(0, 0)
+            nc.vector.tensor_copy(out=columns[:], in_=vector_columns[:, 0:VEC_ROWS])
+            quantise(nc, emb_codes[:], emb_scales[:], emb_grouped[:])
+            take_statistics(0, 1)
+            nc.vector.tensor_scalar_add(out=one_plus_be[:], in0=be_scale, scalar1=1.0)
+            take_statistics(0, 2)
+            nc.vector.tensor_mul(out=gain_bias[:], in0=gain, in1=one_plus_be[:])
+            nc.vector.tensor_mul(out=beta_bias[:], in0=beta, in1=one_plus_be[:])
+            take_statistics(0, 3)
+            nc.vector.tensor_add(out=offset_bias[:], in0=beta_bias[:], in1=be_shift)
+            for j in range(ROWS):
+                aggregate(0, j)
+            finish_statistics(0, on_vector=True)
+            for j in range(ROWS):
+                normalise(0, j)
+
+            interleave_k(nc.scalar.copy, we_grouped[:, D:, :], we_planes[:, :, D:])
+            interleave_k(nc.vector.tensor_copy, we_grouped[:, :D, :], we_planes[:, :, :D])
+            interleave_k(nc.scalar.copy, wo_grouped[:], wo_planes[:])
+            embed(1, m_shift)
+            embed(0, m_scale)
+            for t in range(PACK):
+                nc.scalar.activation(
+                    out=offset_part[:, t, :], in_=m_scale[:, t, :], func=ACT.Identity,
+                    scale=beta[:, t : t + 1], bias=offset_bias[:, t : t + 1],
+                )
+            for t in range(PACK):
+                nc.scalar.activation(
+                    out=mod_gain[:, t, :], in_=m_scale[:, t, :], func=ACT.Identity,
+                    scale=gain[:, t : t + 1], bias=gain_bias[:, t : t + 1],
+                )
+            for j in range(ROWS - 1):
+                take_statistics(1, j)
+            nc.vector.tensor_tensor(
+                out=mod_offset[:], in0=m_shift[:], in1=offset_part[:], op=ALU.add
+            )
+            take_statistics(1, ROWS - 1)
+            for j in range(ROWS):
+                aggregate(1, j)
+            take_statistics(2, 0)
+            finish_statistics(1, on_vector=True)
+            quantise(nc, wo_codes[:], wo_scales[:], wo_grouped[:])
+            for j in range(1, ROWS):
+                take_statistics(2, j)
+            for j in range(ROWS):
+                normalise(1, j, engine=nc.gpsimd if j < 2 else nc.vector)
+            for j in range(ROWS):
+                aggregate(2, j)
+            take_statistics(3, 0)
+            finish_statistics(2, on_vector=True)
+            for j in range(1, ROWS):
+                take_statistics(3, j)
+            for j in range(ROWS):
+                aggregate(3, j)
+            finish_statistics(3, on_vector=True)
+
+        def in_step(step, begin, stage, first=0, end=N_CHUNKS):
             c, part = divmod(step - begin, STEPS)
-            if first_chunk <= c < N_CHUNKS:
+            if first <= c < end:
                 stage(c, part)
 
-        def at_step(step, begin, stage, first_chunk=0):
+        def at_step(step, begin, stage, first=0):
             c, part = divmod(step - begin, STEPS)
-            if part == 0 and first_chunk <= c < N_CHUNKS:
+            if part == 0 and first <= c < N_CHUNKS:
                 stage(c)
 
         with tc.manual_schedule(engines=PINNED):
-            for step in range(STEPS * (N_CHUNKS - 1) + ADD_RESIDUAL + STEPS):
+            for step in range(STEPS * (N_CHUNKS - 1) + ADD_RESIDUAL_DIRECT + STEPS):
                 at_step(step, LOAD_Y, load_y, Y_IN_PROLOGUE)
                 at_step(step, LOAD_X, load_x)
-                in_step(step, ADD_RESIDUAL, add_residual_and_store)
+                if step == LOAD_BO:
+                    nc.sync.dma_start(out=bo_rows[:], in_=bo.partition_broadcast(P))
+                in_step(step, ADD_RESIDUAL, add_residual_and_store, end=DIRECT_FROM)
+                in_step(step, ADD_RESIDUAL_DIRECT, add_residual_and_store, first=DIRECT_FROM)
                 in_step(step, MODULATE, modulate_silu)
                 at_step(step, REGROUP, regroup)
-                in_step(step, PROJECT, project)
+                in_step(step, PROJECT, project, end=DIRECT_FROM)
+                in_step(step, PROJECT, project_direct, first=DIRECT_FROM)
                 in_step(step, TO_K_MAJOR, to_k_major)
-                in_step(step, TO_TOKEN_MAJOR, to_token_major)
-                in_step(step, AGGREGATE, aggregate, STATS_IN_PROLOGUE)
+                in_step(step, TO_TOKEN_MAJOR, to_token_major, end=DIRECT_FROM)
+                in_step(step, AGGREGATE, aggregate, MOMENTS_IN_PROLOGUE)
                 in_step(step, STATISTICS, take_statistics, STATS_IN_PROLOGUE)
                 at_step(step, QUANTISE, quantise_acts)
-                in_step(step, NORMALISE, normalise, STATS_IN_PROLOGUE - 1)
-                at_step(step, FINISH_STATISTICS, finish_statistics, STATS_IN_PROLOGUE)
+                in_step(step, NORMALISE, normalise, NORM_IN_PROLOGUE)
+                in_step(step, ADD_BIAS, add_bias, first=DIRECT_FROM)
+                at_step(step, FINISH_STATISTICS, finish_statistics, MOMENTS_IN_PROLOGUE)

@@ -43,7 +43,7 @@ ADD_BIAS = 5
 ADD_RESIDUAL_DIRECT = 8
 LOAD_BO = 32
 TENSOR_ROWS = (0,)
-WARM_BLOCKS = (0, 2)
+WARM_BLOCKS = (0, 1, 2)
 STATS_IN_PROLOGUE = 4
 MOMENTS_IN_PROLOGUE = 4
 NORM_IN_PROLOGUE = 2

@@ -37,13 +37,10 @@ PROJECT = 7
 TO_TOKEN_MAJOR = 11
 ADD_RESIDUAL = 12
 LOAD_Y = -18
-LOAD_X = 0
-DIRECT_FROM = N_CHUNKS - 3
-ADD_BIAS = 5
-ADD_RESIDUAL_DIRECT = 8
-LOAD_BO = 32
-TENSOR_ROWS = (0,)
-WARM_BLOCKS = (0, 1, 2)
+LOAD_X = -4
+X_CHUNKS_FROM = N_CHUNKS - 2
+X_ROWS = (1, 3)
+WARM_CHUNKS = 2
 STATS_IN_PROLOGUE = 4
 MOMENTS_IN_PROLOGUE = 4
 NORM_IN_PROLOGUE = 2
@@ -87,7 +84,6 @@ def tile_temporalcrossattention_pa_t_kernel(
         stat_pool = ctx.enter_context(tc.tile_pool(name="stat", bufs=4))
         norm_pool = ctx.enter_context(tc.tile_pool(name="norm", bufs=3))
         work = ctx.enter_context(tc.tile_pool(name="work", bufs=2))
-        xb_pool = ctx.enter_context(tc.tile_pool(name="xb", bufs=3))
         out_pool = ctx.enter_context(tc.tile_pool(name="out", bufs=4))
         product_pool = ctx.enter_context(tc.tile_pool(name="product", bufs=3))
         psum = ctx.enter_context(tc.psum_pool(name="psum", bufs=PACK))
@@ -95,7 +91,7 @@ def tile_temporalcrossattention_pa_t_kernel(
 
         y_tiles, x_tiles, stat_tiles, moment_tiles, norm_tiles, k_major_banks = {}, {}, {}, {}, {}, {}
         act_tiles, grouped_tiles, code_tiles, product_tiles = {}, {}, {}, {}
-        token_major_banks, result_tiles, residual_tiles = {}, {}, {}
+        token_major_banks, result_tiles = {}, {}
 
         def load_y(c):
             y_sb = y_pool.tile([P, ROWS, D], BF16)
@@ -144,17 +140,12 @@ def tile_temporalcrossattention_pa_t_kernel(
                 op0=ALU.add, op1=ALU.mult,
             )
 
-        def add_bias(c, j):
-            if j == 0:
-                residual = xb_pool.tile([P, ROWS, D], F32)
-                residual_tiles[c] = residual
-            nc.gpsimd.tensor_tensor(
-                out=residual_tiles[c][:, j, :], in0=x_tiles[c][:, j, :], in1=bo_rows[:], op=ALU.add
-            )
+        def tensor_adds_x(c, j):
+            return c >= X_CHUNKS_FROM and j in X_ROWS
 
         def to_k_major(c, t):
             k_major = psum.tile([P, ROWS, P], F32)
-            if t in WARM_BLOCKS:
+            for repeat in range(2 if c < WARM_CHUNKS else 1):
                 nc.tensor.matmul_mx(
                     out=k_major[:].rearrange("p j q -> p (j q)"),
                     lhsT=we_codes[:, 0:P].bitcast(FP8X4), lhsT_scale=we_scales[:, 0:P],
@@ -211,26 +202,17 @@ def tile_temporalcrossattention_pa_t_kernel(
                 rhs=act_codes[:].bitcast(FP8X4), rhs_scale=act_scales[:],
                 start=True, stop=True,
             )
-            nc.scalar.activation(
-                out=product_tiles[c][:, m, :], in_=acc[:], func=ACT.Identity,
-                bias=columns[:, BO_ROW + m : BO_ROW + m + 1],
-            )
-
-        def project_direct(c, j):
-            act_codes, act_scales = code_tiles[c]
-            tokens = slice(j * P, (j + 1) * P)
-            acc = ring.tile([P, D], F32)
-            nc.tensor.matmul_mx(
-                out=acc[:],
-                lhsT=act_codes[:, tokens].bitcast(FP8X4), lhsT_scale=act_scales[:, tokens],
-                rhs=wo_codes[:].bitcast(FP8X4), rhs_scale=wo_scales[:],
-                start=True, stop=True,
-            )
-            token_major_banks[c, j] = acc
+            bias = columns[:, BO_ROW + m : BO_ROW + m + 1]
+            if c == N_CHUNKS - 1 and m % 2 == 1:
+                nc.vector.tensor_scalar_add(out=product_tiles[c][:, m, :], in0=acc[:], scalar1=bias)
+            else:
+                nc.scalar.activation(
+                    out=product_tiles[c][:, m, :], in_=acc[:], func=ACT.Identity, bias=bias
+                )
 
         def to_token_major(c, j):
             token_major = ring.tile([P, D], F32)
-            if j in TENSOR_ROWS:
+            if tensor_adds_x(c, j):
                 nc.tensor.matmul(
                     out=token_major[:], lhsT=ident_bf16[:], rhs=x_tiles[c][:, j, :],
                     start=True, stop=False,
@@ -238,7 +220,7 @@ def tile_temporalcrossattention_pa_t_kernel(
             for m in range(PACK):
                 columns_of_block = token_major[:, m * P : (m + 1) * P]
                 block = product_tiles[c][:, m, j * P : (j + 1) * P]
-                if j in TENSOR_ROWS:
+                if tensor_adds_x(c, j):
                     nc.tensor.matmul(
                         out=columns_of_block, lhsT=block, rhs=ident_f32[:], is_transpose=True,
                         start=False, stop=m == PACK - 1,
@@ -252,12 +234,11 @@ def tile_temporalcrossattention_pa_t_kernel(
                 result = out_pool.tile([P, ROWS, D], F32)
                 result_tiles[c] = result
             row = result_tiles[c][:, j, :]
-            if c < DIRECT_FROM and j in TENSOR_ROWS:
+            if tensor_adds_x(c, j):
                 nc.scalar.copy(out=row, in_=token_major_banks[c, j][:])
             else:
-                residual = residual_tiles[c] if c >= DIRECT_FROM else x_tiles[c]
                 nc.vector.tensor_tensor(
-                    out=row, in0=token_major_banks[c, j][:], in1=residual[:, j, :], op=ALU.add
+                    out=row, in0=token_major_banks[c, j][:], in1=x_tiles[c][:, j, :], op=ALU.add
                 )
             nc.sync.dma_start(out=out_chunks[c][:, j, :], in_=row)
 
@@ -308,7 +289,6 @@ def tile_temporalcrossattention_pa_t_kernel(
         mod_gain = const.tile([P, PACK, B], F32)
         offset_part = const.tile([P, PACK, B], F32)
         mod_offset = const.tile([P, PACK, B], F32)
-        bo_rows = const.tile([P, D], BF16)
 
         def embed(half, sums):
             columns_of_half = slice(half * D, (half + 1) * D)
@@ -395,10 +375,11 @@ def tile_temporalcrossattention_pa_t_kernel(
             for j in range(ROWS):
                 aggregate(3, j)
             finish_statistics(3, on_vector=True)
+            load_x(0)
 
-        def in_step(step, begin, stage, first=0, end=N_CHUNKS):
+        def in_step(step, begin, stage, first=0):
             c, part = divmod(step - begin, STEPS)
-            if first <= c < end:
+            if first <= c < N_CHUNKS:
                 stage(c, part)
 
         def at_step(step, begin, stage, first=0):
@@ -407,22 +388,17 @@ def tile_temporalcrossattention_pa_t_kernel(
                 stage(c)
 
         with tc.manual_schedule(engines=PINNED):
-            for step in range(STEPS * (N_CHUNKS - 1) + ADD_RESIDUAL_DIRECT + STEPS):
+            for step in range(STEPS * (N_CHUNKS - 1) + ADD_RESIDUAL + STEPS):
                 at_step(step, LOAD_Y, load_y, Y_IN_PROLOGUE)
-                at_step(step, LOAD_X, load_x)
-                if step == LOAD_BO:
-                    nc.sync.dma_start(out=bo_rows[:], in_=bo.partition_broadcast(P))
-                in_step(step, ADD_RESIDUAL, add_residual_and_store, end=DIRECT_FROM)
-                in_step(step, ADD_RESIDUAL_DIRECT, add_residual_and_store, first=DIRECT_FROM)
+                at_step(step, LOAD_X, load_x, first=1)
+                in_step(step, ADD_RESIDUAL, add_residual_and_store)
                 in_step(step, MODULATE, modulate_silu)
                 at_step(step, REGROUP, regroup)
-                in_step(step, PROJECT, project, end=DIRECT_FROM)
-                in_step(step, PROJECT, project_direct, first=DIRECT_FROM)
+                in_step(step, PROJECT, project)
                 in_step(step, TO_K_MAJOR, to_k_major)
-                in_step(step, TO_TOKEN_MAJOR, to_token_major, end=DIRECT_FROM)
+                in_step(step, TO_TOKEN_MAJOR, to_token_major)
                 in_step(step, AGGREGATE, aggregate, MOMENTS_IN_PROLOGUE)
                 in_step(step, STATISTICS, take_statistics, STATS_IN_PROLOGUE)
                 at_step(step, QUANTISE, quantise_acts)
                 in_step(step, NORMALISE, normalise, NORM_IN_PROLOGUE)
-                in_step(step, ADD_BIAS, add_bias, first=DIRECT_FROM)
                 at_step(step, FINISH_STATISTICS, finish_statistics, MOMENTS_IN_PROLOGUE)

@@ -35,7 +35,7 @@ REGROUP = 5
 QUANTISE = 5
 PROJECT = 7
 TO_TOKEN_MAJOR = 11
-ADD_RESIDUAL = 12
+ADD_RESIDUAL = 13
 LOAD_Y = -18
 LOAD_X = -4
 X_CHUNKS_FROM = N_CHUNKS - 2
@@ -86,8 +86,9 @@ def tile_temporalcrossattention_pa_t_kernel(
         work = ctx.enter_context(tc.tile_pool(name="work", bufs=2))
         out_pool = ctx.enter_context(tc.tile_pool(name="out", bufs=4))
         product_pool = ctx.enter_context(tc.tile_pool(name="product", bufs=3))
-        psum = ctx.enter_context(tc.psum_pool(name="psum", bufs=PACK))
+        psum = ctx.enter_context(tc.psum_pool(name="psum", bufs=3))
         ring = ctx.enter_context(tc.psum_pool(name="ring", bufs=2))
+        back = ctx.enter_context(tc.psum_pool(name="back", bufs=3))
 
         y_tiles, x_tiles, stat_tiles, moment_tiles, norm_tiles, k_major_banks = {}, {}, {}, {}, {}, {}
         act_tiles, grouped_tiles, code_tiles, product_tiles = {}, {}, {}, {}
@@ -211,7 +212,7 @@ def tile_temporalcrossattention_pa_t_kernel(
                 )
 
         def to_token_major(c, j):
-            token_major = ring.tile([P, D], F32)
+            token_major = back.tile([P, D], F32)
             if tensor_adds_x(c, j):
                 nc.tensor.matmul(
                     out=token_major[:], lhsT=ident_bf16[:], rhs=x_tiles[c][:, j, :],

from contextlib import ExitStack

import concourse.mybir as mybir
from concourse.masks import make_identity

F32 = mybir.dt.float32
BF16 = mybir.dt.bfloat16
U32 = mybir.dt.uint32
U8 = mybir.dt.uint8
FP8X4 = mybir.dt.float8_e4m3fn_x4
ACT = mybir.ActivationFunctionType
ALU = mybir.AluOpType

P = 128
PACK = 4
B, T, D = 128, 64, 512
EPS = 1e-5

ROWS = 4
CHUNK = P * ROWS
N_CHUNKS = B * T // CHUNK
SEQS = CHUNK // T
SEQ_PARTS = T // ROWS

VECTOR_TOKENS = 3 * P

STEPS = 4
STATISTICS = -13
AGGREGATE = -12
FINISH_STATISTICS = -8
NORMALISE = -6
TO_K_MAJOR = 0
MODULATE = 1
REGROUP = 5
QUANTISE = 5
PROJECT = 7
TO_TOKEN_MAJOR = 11
ADD_RESIDUAL = 13
LOAD_Y = -18
LOAD_X = -4
X_CHUNKS_FROM = N_CHUNKS - 2
X_ROWS = (1, 3)
WARM_CHUNKS = 2
STATS_IN_PROLOGUE = 4
MOMENTS_IN_PROLOGUE = 4
NORM_IN_PROLOGUE = 2
Y_IN_PROLOGUE = 5
PINNED = {
    mybir.EngineType.PE, mybir.EngineType.DVE, mybir.EngineType.Activation, mybir.EngineType.Pool,
}

GAIN_ROW, BETA_ROW, BE_ROW, BO_ROW, VEC_ROWS = 0, 4, 8, 16, 20

FLOPS = 2 * B * T * D * D + 2 * B * D * 2 * D


def interleave_k(copy, grouped, planes):
    copy(
        out=grouped.rearrange("p (c i) t -> p c t i", i=4),
        in_=planes.rearrange("p t (c i) -> p c t i", i=4),
    )


def quantise(nc, codes, scales, grouped):
    nc.vector.quantize_mx(
        out=codes.bitcast(FP8X4),
        scales=scales,
        in_=grouped.rearrange("p w t -> p (w t)"),
    )


def tile_temporalcrossattention_pa_t_kernel(
    tc, x, y, emb0, We, be, ln2_g, ln2_b, Wo, bo, out
):
    nc = tc.nc
    x_chunks = x.flatten_outer_dims().rearrange("(c p j) d -> c p j d", p=P, j=ROWS)
    y_chunks = y.flatten_outer_dims().rearrange("(c p j) d -> c p j d", p=P, j=ROWS)
    out_chunks = out.flatten_outer_dims().rearrange("(c p j) d -> c p j d", p=P, j=ROWS)

    with ExitStack() as ctx:
        const = ctx.enter_context(tc.tile_pool(name="const", bufs=1))
        y_pool = ctx.enter_context(tc.tile_pool(name="y", bufs=6))
        x_pool = ctx.enter_context(tc.tile_pool(name="x", bufs=7))
        stat_pool = ctx.enter_context(tc.tile_pool(name="stat", bufs=4))
        norm_pool = ctx.enter_context(tc.tile_pool(name="norm", bufs=3))
        work = ctx.enter_context(tc.tile_pool(name="work", bufs=2))
        out_pool = ctx.enter_context(tc.tile_pool(name="out", bufs=4))
        product_pool = ctx.enter_context(tc.tile_pool(name="product", bufs=3))
        psum = ctx.enter_context(tc.psum_pool(name="psum", bufs=3))
        ring = ctx.enter_context(tc.psum_pool(name="ring", bufs=2))
        back = ctx.enter_context(tc.psum_pool(name="back", bufs=3))

        y_tiles, x_tiles, stat_tiles, moment_tiles, norm_tiles, k_major_banks = {}, {}, {}, {}, {}, {}
        act_tiles, grouped_tiles, code_tiles, product_tiles = {}, {}, {}, {}
        token_major_banks, result_tiles = {}, {}

        def load_y(c):
            y_sb = y_pool.tile([P, ROWS, D], BF16)
            nc.sync.dma_start(out=y_sb[:], in_=y_chunks[c])
            y_tiles[c] = y_sb

        def load_x(c):
            x_sb = x_pool.tile([P, ROWS, D], BF16)
            nc.sync.dma_start(out=x_sb[:], in_=x_chunks[c])
            x_tiles[c] = x_sb

        def take_statistics(c, j):
            if j == 0:
                stats = stat_pool.tile([P, ROWS, 6], F32)
                mean_var = stat_pool.tile([P, ROWS, 2], F32)
                stat_tiles[c] = (stats, mean_var)
            nc.vector.bn_stats(out=stat_tiles[c][0][:, j, :], in_=y_tiles[c][:, j, :])

        def aggregate(c, j):
            stats, mean_var = stat_tiles[c]
            nc.vector.bn_aggr(out=mean_var[:, j, :], in_=stats[:, j, :])

        def finish_statistics(c, on_vector=False):
            mean_var = stat_tiles[c][1]
            var_eps = stat_pool.tile([P, ROWS], F32)
            neg_mean = stat_pool.tile([P, ROWS], F32)
            rstd = stat_pool.tile([P, ROWS], F32)
            mean, var = mean_var[:, :, 0], mean_var[:, :, 1]
            if on_vector:
                nc.vector.tensor_scalar_add(out=var_eps[:], in0=var, scalar1=EPS)
                nc.vector.tensor_scalar_mul(out=neg_mean[:], in0=mean, scalar1=-1.0)
            else:
                nc.scalar.activation(out=var_eps[:], in_=var, func=ACT.Identity, bias=EPS)
                nc.scalar.activation(out=neg_mean[:], in_=mean, func=ACT.Copy, scale=-1.0)
            nc.gpsimd.tensor_tensor(out=rstd[:], in0=var_eps[:], in1=minus_half[:], op=ALU.pow)
            moment_tiles[c] = (neg_mean, rstd)

        def normalise(c, j, engine=nc.gpsimd):
            if j == 0:
                normed = norm_pool.tile([P, ROWS, D], F32)
                norm_tiles[c] = normed
            neg_mean, rstd = moment_tiles[c]
            engine.tensor_scalar(
                out=norm_tiles[c][:, j, :], in0=y_tiles[c][:, j, :],
                scalar1=neg_mean[:, j : j + 1], scalar2=rstd[:, j : j + 1],
                op0=ALU.add, op1=ALU.mult,
            )

        def tensor_adds_x(c, j):
            return c >= X_CHUNKS_FROM and j in X_ROWS

        def to_k_major(c, t):
            k_major = psum.tile([P, ROWS, P], F32)
            for repeat in range(2 if c < WARM_CHUNKS else 1):
                nc.tensor.matmul_mx(
                    out=k_major[:].rearrange("p j q -> p (j q)"),
                    lhsT=we_codes[:, 0:P].bitcast(FP8X4), lhsT_scale=we_scales[:, 0:P],
                    rhs=we_codes[:, 0:CHUNK].bitcast(FP8X4), rhs_scale=we_scales[:, 0:CHUNK],
                    start=True, stop=True,
                )
            for j in range(ROWS):
                nc.tensor.transpose(
                    out=k_major[:, j, :], in_=norm_tiles[c][:, j, t * P : (t + 1) * P],
                    identity=ident_f32[:],
                )
            k_major_banks[c, t] = k_major

        def modulate_silu(c, t):
            if t == 0:
                acts = work.tile([P, PACK, ROWS, P], BF16)
                act_tiles[c] = acts
            for s in range(SEQS):
                b = c * SEQS + s
                frames = slice(s * SEQ_PARTS, (s + 1) * SEQ_PARTS)
                nc.scalar.activation(
                    out=act_tiles[c][:, t, :, frames], in_=k_major_banks[c, t][:, :, frames],
                    func=ACT.Silu,
                    scale=mod_gain[:, t, b : b + 1], bias=mod_offset[:, t, b : b + 1],
                )

        def regroup(c):
            grouped = work.tile([P, CHUNK, PACK], BF16, align_bytes=64)
            planes = act_tiles[c][:].rearrange("p t j q -> p t (j q)")
            interleave_k(
                nc.vector.tensor_copy, grouped[:, :VECTOR_TOKENS, :], planes[:, :, :VECTOR_TOKENS]
            )
            interleave_k(
                nc.scalar.copy, grouped[:, VECTOR_TOKENS:, :], planes[:, :, VECTOR_TOKENS:]
            )
            grouped_tiles[c] = grouped

        def quantise_acts(c):
            act_codes = work.tile([P, CHUNK], U32, align_bytes=64)
            act_scales = work.tile([P, CHUNK], U8, align_bytes=64)
            quantise(nc, act_codes[:], act_scales[:], grouped_tiles[c][:])
            code_tiles[c] = (act_codes, act_scales)

        def project(c, m):
            if m == 0:
                product = product_pool.tile([P, PACK, CHUNK], F32)
                product_tiles[c] = product
            act_codes, act_scales = code_tiles[c]
            features = slice(m * P, (m + 1) * P)
            acc = ring.tile([P, CHUNK], F32)
            nc.tensor.matmul_mx(
                out=acc[:],
                lhsT=wo_codes[:, features].bitcast(FP8X4), lhsT_scale=wo_scales[:, features],
                rhs=act_codes[:].bitcast(FP8X4), rhs_scale=act_scales[:],
                start=True, stop=True,
            )
            bias = columns[:, BO_ROW + m : BO_ROW + m + 1]
            if c == N_CHUNKS - 1 and m % 2 == 1:
                nc.vector.tensor_scalar_add(out=product_tiles[c][:, m, :], in0=acc[:], scalar1=bias)
            else:
                nc.scalar.activation(
                    out=product_tiles[c][:, m, :], in_=acc[:], func=ACT.Identity, bias=bias
                )

        def to_token_major(c, j):
            token_major = back.tile([P, D], F32)
            if tensor_adds_x(c, j):
                nc.tensor.matmul(
                    out=token_major[:], lhsT=ident_bf16[:], rhs=x_tiles[c][:, j, :],
                    start=True, stop=False,
                )
            for m in range(PACK):
                columns_of_block = token_major[:, m * P : (m + 1) * P]
                block = product_tiles[c][:, m, j * P : (j + 1) * P]
                if tensor_adds_x(c, j):
                    nc.tensor.matmul(
                        out=columns_of_block, lhsT=block, rhs=ident_f32[:], is_transpose=True,
                        start=False, stop=m == PACK - 1,
                    )
                else:
                    nc.tensor.transpose(out=columns_of_block, in_=block, identity=ident_f32[:])
            token_major_banks[c, j] = token_major

        def add_residual_and_store(c, j):
            if j == 0:
                result = out_pool.tile([P, ROWS, D], F32)
                result_tiles[c] = result
            row = result_tiles[c][:, j, :]
            if tensor_adds_x(c, j):
                nc.scalar.copy(out=row, in_=token_major_banks[c, j][:])
            else:
                nc.vector.tensor_tensor(
                    out=row, in0=token_major_banks[c, j][:], in1=x_tiles[c][:, j, :], op=ALU.add
                )
            nc.sync.dma_start(out=out_chunks[c][:, j, :], in_=row)

        emb_sb = const.tile([P, D], BF16)
        nc.sync.dma_start(out=emb_sb[:], in_=emb0)
        vector_rows = const.tile([P, P], BF16)
        nc.vector.memset(vector_rows[:], 0.0)
        for first_row, vector in ((GAIN_ROW, ln2_g), (BETA_ROW, ln2_b), (BE_ROW, be), (BO_ROW, bo)):
            rows = vector.rearrange("(r q) -> r q", q=P)
            nc.sync.dma_start(out=vector_rows[first_row : first_row + rows.shape[0], :], in_=rows)
        load_y(0)
        we_planes = const.tile([P, PACK, 2 * D], BF16)
        nc.sync.dma_start(out=we_planes[:], in_=We.rearrange("(t p) n -> p t n", p=P))
        load_y(1)
        wo_planes = const.tile([P, PACK, D], BF16)
        nc.sync.dma_start(out=wo_planes[:], in_=Wo.rearrange("(t p) n -> p t n", p=P))
        for c in range(2, Y_IN_PROLOGUE):
            load_y(c)

        ident_bf16 = const.tile([P, P], BF16)
        make_identity(nc, ident_bf16[:])
        ident_f32 = const.tile([P, P], F32)
        make_identity(nc, ident_f32[:])
        minus_half = const.tile([P, ROWS], F32)
        nc.gpsimd.memset(minus_half[:], -0.5)

        emb_act = const.tile([P, D], BF16)
        emb_grouped = const.tile([P, B, PACK], BF16, align_bytes=64)
        emb_codes = const.tile([P, B], U32, align_bytes=64)
        emb_scales = const.tile([P, B], U8, align_bytes=64)
        columns = const.tile([P, VEC_ROWS], F32)
        gain = columns[:, GAIN_ROW : GAIN_ROW + PACK]
        beta = columns[:, BETA_ROW : BETA_ROW + PACK]
        be_scale = columns[:, BE_ROW : BE_ROW + PACK]
        be_shift = columns[:, BE_ROW + PACK : BE_ROW + 2 * PACK]
        one_plus_be = const.tile([P, PACK], F32)
        gain_bias = const.tile([P, PACK], F32)
        beta_bias = const.tile([P, PACK], F32)
        offset_bias = const.tile([P, PACK], F32)
        we_grouped = const.tile([P, 2 * D, PACK], BF16, align_bytes=64)
        we_codes = const.tile([P, 2 * D], U32, align_bytes=64)
        we_scales = const.tile([P, 2 * D], U8, align_bytes=64)
        wo_grouped = const.tile([P, D, PACK], BF16, align_bytes=64)
        wo_codes = const.tile([P, D], U32, align_bytes=64)
        wo_scales = const.tile([P, D], U8, align_bytes=64)
        m_scale = ring.tile([P, PACK, B], F32, tag="acc")
        m_shift = ring.tile([P, PACK, B], F32, tag="acc")
        mod_gain = const.tile([P, PACK, B], F32)
        offset_part = const.tile([P, PACK, B], F32)
        mod_offset = const.tile([P, PACK, B], F32)

        def embed(half, sums):
            columns_of_half = slice(half * D, (half + 1) * D)
            quantise(
                nc, we_codes[:, columns_of_half], we_scales[:, columns_of_half],
                we_grouped[:, columns_of_half, :],
            )
            for t in range(PACK):
                features = slice((half * PACK + t) * P, (half * PACK + t + 1) * P)
                nc.tensor.matmul_mx(
                    out=sums[:, t, :],
                    lhsT=we_codes[:, features].bitcast(FP8X4), lhsT_scale=we_scales[:, features],
                    rhs=emb_codes[:].bitcast(FP8X4), rhs_scale=emb_scales[:],
                    start=True, stop=True,
                )

        with tc.manual_schedule(engines=PINNED):
            nc.scalar.activation(out=emb_act[:], in_=emb_sb[:], func=ACT.Silu)
            emb_k_major = psum.tile([P, PACK, P], BF16, tag="k_major")
            for t in range(PACK):
                nc.tensor.transpose(
                    out=emb_k_major[:, t, :], in_=emb_act[:, t * P : (t + 1) * P],
                    identity=ident_bf16[:],
                )
            vector_columns = psum.tile([P, P], BF16, tag="k_major")
            nc.tensor.transpose(
                out=vector_columns[:], in_=vector_rows[:], identity=ident_bf16[:]
            )
            nc.vector.tensor_copy(
                out=emb_grouped[:], in_=emb_k_major[:].rearrange("p t b -> p b t")
            )
            take_statistics(0, 0)
            nc.vector.tensor_copy(out=columns[:], in_=vector_columns[:, 0:VEC_ROWS])
            quantise(nc, emb_codes[:], emb_scales[:], emb_grouped[:])
            take_statistics(0, 1)
            nc.vector.tensor_scalar_add(out=one_plus_be[:], in0=be_scale, scalar1=1.0)
            take_statistics(0, 2)
            nc.vector.tensor_mul(out=gain_bias[:], in0=gain, in1=one_plus_be[:])
            nc.vector.tensor_mul(out=beta_bias[:], in0=beta, in1=one_plus_be[:])
            take_statistics(0, 3)
            nc.vector.tensor_add(out=offset_bias[:], in0=beta_bias[:], in1=be_shift)
            for j in range(ROWS):
                aggregate(0, j)
            finish_statistics(0, on_vector=True)
            for j in range(ROWS):
                normalise(0, j)

            interleave_k(nc.scalar.copy, we_grouped[:, D:, :], we_planes[:, :, D:])
            interleave_k(nc.vector.tensor_copy, we_grouped[:, :D, :], we_planes[:, :, :D])
            interleave_k(nc.scalar.copy, wo_grouped[:], wo_planes[:])
            embed(1, m_shift)
            embed(0, m_scale)
            for t in range(PACK):
                nc.scalar.activation(
                    out=offset_part[:, t, :], in_=m_scale[:, t, :], func=ACT.Identity,
                    scale=beta[:, t : t + 1], bias=offset_bias[:, t : t + 1],
                )
            for t in range(PACK):
                nc.scalar.activation(
                    out=mod_gain[:, t, :], in_=m_scale[:, t, :], func=ACT.Identity,
                    scale=gain[:, t : t + 1], bias=gain_bias[:, t : t + 1],
                )
            for j in range(ROWS - 1):
                take_statistics(1, j)
            nc.vector.tensor_tensor(
                out=mod_offset[:], in0=m_shift[:], in1=offset_part[:], op=ALU.add
            )
            take_statistics(1, ROWS - 1)
            for j in range(ROWS):
                aggregate(1, j)
            take_statistics(2, 0)
            finish_statistics(1, on_vector=True)
            quantise(nc, wo_codes[:], wo_scales[:], wo_grouped[:])
            for j in range(1, ROWS):
                take_statistics(2, j)
            for j in range(ROWS):
                normalise(1, j, engine=nc.gpsimd if j < 2 else nc.vector)
            for j in range(ROWS):
                aggregate(2, j)
            take_statistics(3, 0)
            finish_statistics(2, on_vector=True)
            for j in range(1, ROWS):
                take_statistics(3, j)
            for j in range(ROWS):
                aggregate(3, j)
            finish_statistics(3, on_vector=True)
            load_x(0)

        def in_step(step, begin, stage, first=0):
            c, part = divmod(step - begin, STEPS)
            if first <= c < N_CHUNKS:
                stage(c, part)

        def at_step(step, begin, stage, first=0):
            c, part = divmod(step - begin, STEPS)
            if part == 0 and first <= c < N_CHUNKS:
                stage(c)

        with tc.manual_schedule(engines=PINNED):
            for step in range(STEPS * (N_CHUNKS - 1) + ADD_RESIDUAL + STEPS):
                at_step(step, LOAD_Y, load_y, Y_IN_PROLOGUE)
                at_step(step, LOAD_X, load_x, first=1)
                in_step(step, ADD_RESIDUAL, add_residual_and_store)
                in_step(step, MODULATE, modulate_silu)
                at_step(step, REGROUP, regroup)
                in_step(step, PROJECT, project)
                in_step(step, TO_K_MAJOR, to_k_major)
                in_step(step, TO_TOKEN_MAJOR, to_token_major)
                in_step(step, AGGREGATE, aggregate, MOMENTS_IN_PROLOGUE)
                in_step(step, STATISTICS, take_statistics, STATS_IN_PROLOGUE)
                at_step(step, QUANTISE, quantise_acts)
                in_step(step, NORMALISE, normalise, NORM_IN_PROLOGUE)
                at_step(step, FINISH_STATISTICS, finish_statistics, MOMENTS_IN_PROLOGUE)
